import numpy as np
import ml_dtypes


def mxq(x, axis, fmt="e4m3"):
    dtype, down = {"e4m3": (ml_dtypes.float8_e4m3fn, 7), "e5m2": (ml_dtypes.float8_e5m2, 14)}[fmt]
    v = np.moveaxis(np.asarray(x, np.float32).astype(ml_dtypes.bfloat16).astype(np.float64), axis, -1)
    blocks = v.reshape(v.shape[:-1] + (-1, 32))
    amax = np.abs(blocks).max(-1, keepdims=True)
    byte = np.maximum(np.where(amax > 0, np.frexp(amax)[1] - 1 + 127, 0) - down, 1)
    scale = np.exp2(byte - 127.0)
    codes = (blocks / scale).astype(np.float32).astype(dtype).astype(np.float64)
    return np.moveaxis((codes * scale).reshape(v.shape), -1, axis)


WIDE = False


def mx_kscale(k):
    if not WIDE:
        return np.ones(k)
    levels = np.array([10, -10, 5, -5, 0])
    a = np.random.permutation(np.resize(levels, k // 512 * 4)).reshape(k // 512, 4)
    idx = np.arange(k)
    return np.exp2(a[idx // 512, idx % 128 // 32])


BF16 = ml_dtypes.bfloat16


def bf(x):
    return np.asarray(x, np.float32).astype(BF16)


def f64(x):
    return np.asarray(x).astype(np.float64)


B, HP, WP, E, F, NH, WS = 2, 32, 64, 1024, 2048, 16, 8
NWH, NWW = HP // WS, WP // WS
L, N = B * NWH * NWW, WS * WS
LN_EPS = 1e-5


def layernorm(x, g, b):
    mu = x.mean(-1, keepdims=True)
    var = ((x - mu) ** 2).mean(-1, keepdims=True)
    return (x - mu) / np.sqrt(var + LN_EPS) * g + b


def setup_inputs():
    s = mx_kscale(E)
    return {"x": bf(np.random.standard_normal((B, HP * WP, E))),
            "o": bf(np.random.standard_normal((L, N, E)) * 0.5 * s),
            "out_w": bf(np.random.standard_normal((E, E)) * 2.0 / np.sqrt(E) / s),
            "out_b": bf(np.random.standard_normal(E) * 0.2),
            "ln1_g": bf(1.0 + 0.1 * np.random.standard_normal(E)),
            "ln1_b": bf(np.random.standard_normal(E) * 0.2)}


def reference(x, o, out_w, out_b, ln1_g, ln1_b):
    xw = f64(x).reshape(B, NWH, WS, NWW, WS, E).transpose(0, 1, 3, 2, 4, 5).reshape(L, N, E)
    attn_out = (mxq(f64(o), 2, "e4m3") @ mxq(f64(out_w), 1, "e4m3").T) + f64(out_b)
    return layernorm(xw + attn_out, f64(ln1_g), f64(ln1_b))

@@ -1,0 +1,262 @@
+from contextlib import ExitStack
+
+import concourse.mybir as mybir
+from concourse.masks import make_identity
+
+F32 = mybir.dt.float32
+BF16 = mybir.dt.bfloat16
+U32 = mybir.dt.uint32
+U8 = mybir.dt.uint8
+FP8X4 = mybir.dt.float8_e4m3fn_x4
+ALU = mybir.AluOpType
+ACT = mybir.ActivationFunctionType
+
+P = 128
+E = 1024
+N_TOKENS = 4096
+BAND_TOKENS = 512
+BAND_TILES = BAND_TOKENS // P
+N_BANDS = N_TOKENS // BAND_TOKENS
+N_TILES = N_TOKENS // P
+PACK = 4
+PASSES = E // (P * PACK)
+WORD_BLOCKS = E // 2 // P
+BANK = 512
+HALVES = E // BANK
+C_TILES = E // P
+LN_EPS = 1e-5
+
+TRANSPOSE_LEAD = 5
+BIAS_LEAD = 2
+LOAD_LEAD = 3
+
+FLOPS = 2 * N_TOKENS * E * E
+
+
+def half(h):
+    return slice(h * BANK, (h + 1) * BANK)
+
+
+def tile_swintransformerblock_pa_t_kernel(tc, x, o, out_w, out_b, ln1_g, ln1_b, out):
+    nc = tc.nc
+    x_tok = x.rearrange("b t e -> (b t) e")
+    o_tok = o.rearrange("l n e -> (l n) e")
+    out_tok = out.rearrange("l n e -> (l n) e")
+
+    with ExitStack() as ctx:
+        consts = ctx.enter_context(tc.tile_pool(name="consts", bufs=1))
+        weights = ctx.enter_context(tc.tile_pool(name="weights", bufs=1))
+        bands = ctx.enter_context(tc.tile_pool(name="bands", bufs=LOAD_LEAD))
+        operands = ctx.enter_context(tc.tile_pool(name="operands", bufs=2))
+        work = ctx.enter_context(tc.tile_pool(name="work", bufs=4))
+        small = ctx.enter_context(tc.tile_pool(name="small", bufs=4))
+        const_ps = ctx.enter_context(tc.psum_pool(name="const_ps", bufs=1))
+        acc_ps = ctx.enter_context(tc.psum_pool(name="acc_ps", bufs=1))
+        turn_ps = ctx.enter_context(tc.psum_pool(name="turn_ps", bufs=2))
+        ctx.enter_context(tc.manual_schedule())
+
+        o_bands = {}
+        x_bands = {}
+
+        def load_band(band):
+            tokens = slice(band * BAND_TOKENS, (band + 1) * BAND_TOKENS)
+            o_band = bands.tile([P, BAND_TILES, E], BF16, tag="o_band")
+            nc.sync.dma_start(
+                out=o_band[:], in_=o_tok[tokens, :].rearrange("(p j) e -> p j e", j=BAND_TILES)
+            )
+            x_band = bands.tile([P, BAND_TILES, E], BF16, tag="x_band")
+            x_runs = x_tok[tokens, :].rearrange(
+                "(r w h j) e -> h w r (j e)", r=8, w=8, h=2, j=BAND_TILES
+            )
+            for h in range(2):
+                nc.sync.dma_start(
+                    out=x_band[h:P:2, :, :].rearrange("q j e -> q (j e)"), in_=x_runs[h]
+                )
+            o_bands[band] = o_band
+            x_bands[band] = x_band
+
+        vectors = consts.tile([1, 3, E], BF16)
+        for v, vec in enumerate((ln1_g, ln1_b, out_b)):
+            nc.sync.dma_start(out=vectors[0:1, v, :], in_=vec.rearrange("(a e) -> a e", a=1))
+        w_raw = weights.tile([P, C_TILES, E], BF16)
+        w_view = out_w.rearrange("(c p) k -> p c k", p=P)
+        for h in range(HALVES):
+            blocks = slice(h * C_TILES // HALVES, (h + 1) * C_TILES // HALVES)
+            nc.sync.dma_start(out=w_raw[:, blocks, :], in_=w_view[:, blocks, :])
+        for band in range(LOAD_LEAD):
+            load_band(band)
+
+        ident = consts.tile([P, P], F32)
+        make_identity(nc, ident[:])
+        ones = consts.tile([P, P], BF16)
+        nc.vector.memset(ones[:], 1.0)
+        eps = consts.tile([P, 1], F32)
+        nc.vector.memset(eps[:], LN_EPS)
+        warm = consts.tile([P, 1], F32)
+        nc.scalar.activation(out=warm[:], in_=eps[:], func=ACT.Abs_reciprocal_sqrt)
+
+        rows = consts.tile([P, 3, E], BF16)
+        nc.vector.memset(rows[:], 0.0)
+        nc.vector.tensor_copy(out=rows[0:1, :, :], in_=vectors[:])
+        gain_ps = [const_ps.tile([P, BANK], F32, name="gain_ps%d" % h) for h in range(HALVES)]
+        shift_ps = [const_ps.tile([P, BANK], F32, name="shift_ps%d" % h) for h in range(HALVES)]
+        bias_bc = consts.tile([P, E], BF16)
+        for h in range(HALVES):
+            nc.tensor.matmul(out=gain_ps[h][:], lhsT=ones[:], rhs=rows[:, 0, half(h)], start=True, stop=True)
+            nc.tensor.matmul(out=shift_ps[h][:], lhsT=ones[:], rhs=rows[:, 1, half(h)], start=True, stop=True)
+            bias_ps = acc_ps.tile([P, BANK], F32, tag="acc%d" % h)
+            nc.tensor.matmul(out=bias_ps[:], lhsT=ones[:], rhs=rows[:, 2, half(h)], start=True, stop=True)
+            nc.scalar.copy(out=bias_bc[:, half(h)], in_=bias_ps[:])
+
+        w_words = w_raw[:].bitcast(F32)
+        w_grouped = weights.tile([P, PASSES, E, PACK], BF16, align_bytes=64)
+        w_grouped_words = w_grouped[:].bitcast(F32)
+        w_codes = weights.tile([P, PASSES, E], U32, align_bytes=64)
+        w_scales = weights.tile([P, PASSES, E], U8, align_bytes=64)
+        for h in range(HALVES):
+            for c in range(h * C_TILES // HALVES, (h + 1) * C_TILES // HALVES):
+                turned = turn_ps.tile([P, WORD_BLOCKS, P], F32, tag="turned")
+                for b in range(WORD_BLOCKS):
+                    nc.tensor.transpose(turned[:, b, :], w_words[:, c, b * P : (b + 1) * P], ident[:])
+                copy = nc.scalar.copy if c % 2 == 0 else nc.vector.tensor_copy
+                copy(
+                    out=w_grouped_words[:, :, c * P : (c + 1) * P, :],
+                    in_=turned[:].rearrange("p (g u) c -> p g c u", u=2),
+                )
+            for g in range(PASSES):
+                nc.vector.quantize_mx(
+                    out=w_codes[:, g, half(h)].bitcast(FP8X4),
+                    scales=w_scales[:, g, half(h)],
+                    in_=w_grouped[:, g, half(h), :].rearrange("p c f -> p (c f)"),
+                )
+
+        grouped = {}
+        o_codes = {}
+        o_scales = {}
+        x_bias = {}
+        acc = {}
+        resid = {}
+        neg_mean = {}
+        rstd = {}
+
+        def transpose_tile(i):
+            band, j = divmod(i, BAND_TILES)
+            if j == 0:
+                grouped[band] = operands.tile(
+                    [P, BAND_TILES, PASSES, P, PACK], BF16, tag="grouped", name="grouped", align_bytes=64
+                )
+            turned = turn_ps.tile([P, WORD_BLOCKS, P], F32, tag="turned")
+            o_words = o_bands[band][:].bitcast(F32)
+            for b in range(WORD_BLOCKS):
+                nc.tensor.transpose(turned[:, b, :], o_words[:, j, b * P : (b + 1) * P], ident[:])
+            nc.scalar.copy(
+                out=grouped[band][:].bitcast(F32)[:, j],
+                in_=turned[:].rearrange("p (g u) t -> p g t u", u=2),
+            )
+
+        def quantise_band(band):
+            codes = operands.tile([P, BAND_TILES * PASSES * P], U32, tag="codes", align_bytes=64)
+            scales = operands.tile([P, BAND_TILES * PASSES * P], U8, tag="scales", align_bytes=64)
+            nc.vector.quantize_mx(
+                out=codes[:].bitcast(FP8X4),
+                scales=scales[:],
+                in_=grouped[band][:].rearrange("p j g t f -> p (j g t f)"),
+            )
+            o_codes[band] = codes
+            o_scales[band] = scales
+
+        def add_bias(i):
+            band, j = divmod(i, BAND_TILES)
+            xb = work.tile([P, E], F32, tag="x_bias")
+            nc.gpsimd.tensor_tensor(out=xb[:], in0=x_bands[band][:, j, :], in1=bias_bc[:], op=ALU.add)
+            x_bias[i] = xb
+
+        def matmul_tile(i):
+            band, j = divmod(i, BAND_TILES)
+            acc[i] = []
+            for h in range(HALVES):
+                bank = acc_ps.tile([P, BANK], F32, tag="acc%d" % h)
+                for g in range(PASSES):
+                    cols = slice((j * PASSES + g) * P, (j * PASSES + g + 1) * P)
+                    nc.tensor.matmul_mx(
+                        out=bank[:],
+                        lhsT=o_codes[band][:, cols].bitcast(FP8X4),
+                        lhsT_scale=o_scales[band][:, cols],
+                        rhs=w_codes[:, g, half(h)].bitcast(FP8X4),
+                        rhs_scale=w_scales[:, g, half(h)],
+                        start=(g == 0),
+                        stop=(g == PASSES - 1),
+                    )
+                acc[i].append(bank)
+
+        def residual_tile(i):
+            r = work.tile([P, E], F32, tag="resid")
+            sums = small.tile([P, HALVES], F32, tag="sums")
+            for h in range(HALVES):
+                nc.vector.scalar_tensor_tensor(
+                    out=r[:, half(h)],
+                    in0=acc[i][h][:],
+                    scalar=1.0,
+                    in1=x_bias[i][:, half(h)],
+                    op0=ALU.mult,
+                    op1=ALU.add,
+                    accum_out=sums[:, h : h + 1],
+                )
+            resid[i] = r
+            return sums
+
+        def stats_tile(i, sums):
+            scaled = small.tile([P, HALVES], F32, tag="scaled")
+            nm = small.tile([P, 1], F32, tag="neg_mean")
+            nc.scalar.activation(out=scaled[:], in_=sums[:], func=ACT.Identity, scale=-1.0 / E, accum_out=nm[:])
+            squares = work.tile([P, E], BF16, tag="squares")
+            ssq = small.tile([P, 1], F32, tag="ssq")
+            nc.scalar.activation(out=squares[:], in_=resid[i][:], func=ACT.Square, bias=nm[:], accum_out=ssq[:])
+            rs = small.tile([P, 1], F32, tag="rstd")
+            nc.scalar.activation(out=rs[:], in_=ssq[:], func=ACT.Abs_reciprocal_sqrt, bias=eps[:], scale=1.0 / E)
+            neg_mean[i] = nm
+            rstd[i] = rs
+
+        def affine_tile(i):
+            band, j = divmod(i, BAND_TILES)
+            y = work.tile([P, E], F32, tag="y")
+            for h in range(HALVES):
+                nc.vector.scalar_tensor_tensor(
+                    out=y[:, half(h)],
+                    in0=resid[i][:, half(h)],
+                    scalar=neg_mean[i][:],
+                    in1=gain_ps[h][:],
+                    op0=ALU.add,
+                    op1=ALU.mult,
+                )
+            for h in range(HALVES):
+                nc.vector.scalar_tensor_tensor(
+                    out=y[:, half(h)],
+                    in0=y[:, half(h)],
+                    scalar=rstd[i][:],
+                    in1=shift_ps[h][:],
+                    op0=ALU.mult,
+                    op1=ALU.add,
+                )
+            tokens = slice(band * BAND_TOKENS, (band + 1) * BAND_TOKENS)
+            nc.sync.dma_start(
+                out=out_tok[tokens, :].rearrange("(p j) e -> p j e", j=BAND_TILES)[:, j, :], in_=y[:]
+            )
+
+        for s in range(-TRANSPOSE_LEAD, N_TILES + 1):
+            if s + TRANSPOSE_LEAD < N_TILES:
+                transpose_tile(s + TRANSPOSE_LEAD)
+            if 0 <= s + 1 < N_TILES and (s + 1) % BAND_TILES == 0:
+                quantise_band((s + 1) // BAND_TILES)
+            if 0 <= s + BIAS_LEAD < N_TILES:
+                add_bias(s + BIAS_LEAD)
+            if 0 <= s < N_TILES:
+                sums = residual_tile(s)
+            if 0 <= s + 1 < N_TILES:
+                matmul_tile(s + 1)
+            if 0 <= s < N_TILES:
+                stats_tile(s, sums)
+            if 0 <= s - 1:
+                affine_tile(s - 1)
+            if s >= 0 and s % BAND_TILES == 2 and s // BAND_TILES + LOAD_LEAD < N_BANDS:
+                load_band(s // BAND_TILES + LOAD_LEAD)

@@ -49,6 +49,7 @@ def tile_swintransformerblock_pa_t_kernel(tc, x, o, out_w, out_b, ln1_g, ln1_b, 
         bands = ctx.enter_context(tc.tile_pool(name="bands", bufs=LOAD_LEAD))
         operands = ctx.enter_context(tc.tile_pool(name="operands", bufs=2))
         work = ctx.enter_context(tc.tile_pool(name="work", bufs=4))
+        biased = ctx.enter_context(tc.tile_pool(name="biased", bufs=BIAS_LEAD))
         small = ctx.enter_context(tc.tile_pool(name="small", bufs=4))
         const_ps = ctx.enter_context(tc.psum_pool(name="const_ps", bufs=1))
         acc_ps = ctx.enter_context(tc.psum_pool(name="acc_ps", bufs=1))
@@ -138,6 +139,8 @@ def tile_swintransformerblock_pa_t_kernel(tc, x, o, out_w, out_b, ln1_g, ln1_b, 
         resid = {}
         neg_mean = {}
         rstd = {}
+        neg_mean_rstd = {}
+        normed = {}
 
         def transpose_tile(i):
             band, j = divmod(i, BAND_TILES)
@@ -149,6 +152,10 @@ def tile_swintransformerblock_pa_t_kernel(tc, x, o, out_w, out_b, ln1_g, ln1_b, 
             o_words = o_bands[band][:].bitcast(F32)
             for b in range(WORD_BLOCKS):
                 nc.tensor.transpose(turned[:, b, :], o_words[:, j, b * P : (b + 1) * P], ident[:])
+            return turned
+
+        def regroup_tile(i, turned):
+            band, j = divmod(i, BAND_TILES)
             nc.scalar.copy(
                 out=grouped[band][:].bitcast(F32)[:, j],
                 in_=turned[:].rearrange("p (g u) t -> p g t u", u=2),
@@ -167,7 +174,7 @@ def tile_swintransformerblock_pa_t_kernel(tc, x, o, out_w, out_b, ln1_g, ln1_b, 
 
         def add_bias(i):
             band, j = divmod(i, BAND_TILES)
-            xb = work.tile([P, E], F32, tag="x_bias")
+            xb = biased.tile([P, E], F32, tag="x_bias")
             nc.gpsimd.tensor_tensor(out=xb[:], in0=x_bands[band][:, j, :], in1=bias_bc[:], op=ALU.add)
             x_bias[i] = xb
 
@@ -205,58 +212,69 @@ def tile_swintransformerblock_pa_t_kernel(tc, x, o, out_w, out_b, ln1_g, ln1_b, 
             resid[i] = r
             return sums
 
-        def stats_tile(i, sums):
+        def mean_tile(i, sums):
             scaled = small.tile([P, HALVES], F32, tag="scaled")
             nm = small.tile([P, 1], F32, tag="neg_mean")
             nc.scalar.activation(out=scaled[:], in_=sums[:], func=ACT.Identity, scale=-1.0 / E, accum_out=nm[:])
+            neg_mean[i] = nm
+
+        def squares_tile(i):
             squares = work.tile([P, E], BF16, tag="squares")
             ssq = small.tile([P, 1], F32, tag="ssq")
-            nc.scalar.activation(out=squares[:], in_=resid[i][:], func=ACT.Square, bias=nm[:], accum_out=ssq[:])
+            nc.scalar.activation(
+                out=squares[:], in_=resid[i][:], func=ACT.Square, bias=neg_mean[i][:], accum_out=ssq[:]
+            )
+            return ssq
+
+        def rstd_tile(i, ssq):
             rs = small.tile([P, 1], F32, tag="rstd")
             nc.scalar.activation(out=rs[:], in_=ssq[:], func=ACT.Abs_reciprocal_sqrt, bias=eps[:], scale=1.0 / E)
-            neg_mean[i] = nm
+            nb = small.tile([P, 1], F32, tag="neg_mean_rstd")
+            nc.scalar.activation(out=nb[:], in_=neg_mean[i][:], func=ACT.Copy, scale=rs[:])
             rstd[i] = rs
+            neg_mean_rstd[i] = nb
+
+        def normalise_tile(i):
+            y = work.tile([P, E], F32, tag="y")
+            nc.scalar.activation(
+                out=y[:], in_=resid[i][:], func=ACT.Identity, scale=rstd[i][:], bias=neg_mean_rstd[i][:]
+            )
+            normed[i] = y
 
         def affine_tile(i):
             band, j = divmod(i, BAND_TILES)
-            y = work.tile([P, E], F32, tag="y")
+            y = normed[i]
             for h in range(HALVES):
-                nc.vector.scalar_tensor_tensor(
-                    out=y[:, half(h)],
-                    in0=resid[i][:, half(h)],
-                    scalar=neg_mean[i][:],
-                    in1=gain_ps[h][:],
-                    op0=ALU.add,
-                    op1=ALU.mult,
-                )
+                nc.vector.tensor_tensor(out=y[:, half(h)], in0=y[:, half(h)], in1=gain_ps[h][:], op=ALU.mult)
             for h in range(HALVES):
-                nc.vector.scalar_tensor_tensor(
-                    out=y[:, half(h)],
-                    in0=y[:, half(h)],
-                    scalar=rstd[i][:],
-                    in1=shift_ps[h][:],
-                    op0=ALU.mult,
-                    op1=ALU.add,
-                )
+                nc.vector.tensor_tensor(out=y[:, half(h)], in0=y[:, half(h)], in1=shift_ps[h][:], op=ALU.add)
             tokens = slice(band * BAND_TOKENS, (band + 1) * BAND_TOKENS)
             nc.sync.dma_start(
                 out=out_tok[tokens, :].rearrange("(p j) e -> p j e", j=BAND_TILES)[:, j, :], in_=y[:]
             )
 
-        for s in range(-TRANSPOSE_LEAD, N_TILES + 1):
+        for s in range(-TRANSPOSE_LEAD, N_TILES + 2):
             if s + TRANSPOSE_LEAD < N_TILES:
-                transpose_tile(s + TRANSPOSE_LEAD)
+                turned = transpose_tile(s + TRANSPOSE_LEAD)
             if 0 <= s + 1 < N_TILES and (s + 1) % BAND_TILES == 0:
                 quantise_band((s + 1) // BAND_TILES)
-            if 0 <= s + BIAS_LEAD < N_TILES:
-                add_bias(s + BIAS_LEAD)
             if 0 <= s < N_TILES:
                 sums = residual_tile(s)
+            if 0 <= s + BIAS_LEAD < N_TILES:
+                add_bias(s + BIAS_LEAD)
             if 0 <= s + 1 < N_TILES:
                 matmul_tile(s + 1)
             if 0 <= s < N_TILES:
-                stats_tile(s, sums)
-            if 0 <= s - 1:
-                affine_tile(s - 1)
+                mean_tile(s, sums)
+            if s + TRANSPOSE_LEAD < N_TILES:
+                regroup_tile(s + TRANSPOSE_LEAD, turned)
+            if 0 <= s < N_TILES:
+                ssq = squares_tile(s)
+            if 0 <= s - 1 < N_TILES:
+                normalise_tile(s - 1)
+            if 0 <= s < N_TILES:
+                rstd_tile(s, ssq)
+            if 0 <= s - 2:
+                affine_tile(s - 2)
             if s >= 0 and s % BAND_TILES == 2 and s // BAND_TILES + LOAD_LEAD < N_BANDS:
                 load_band(s // BAND_TILES + LOAD_LEAD)

@@ -70,7 +70,7 @@ def tile_swintransformerblock_pa_t_kernel(tc, x, o, out_w, out_b, ln1_g, ln1_b, 
                 "(r w h j) e -> h w r (j e)", r=8, w=8, h=2, j=BAND_TILES
             )
             for h in range(2):
-                nc.sync.dma_start(
+                nc.gpsimd.dma_start(
                     out=x_band[h:P:2, :, :].rearrange("q j e -> q (j e)"), in_=x_runs[h]
                 )
             o_bands[band] = o_band

@@ -70,7 +70,7 @@ def tile_swintransformerblock_pa_t_kernel(tc, x, o, out_w, out_b, ln1_g, ln1_b, 
                 "(r w h j) e -> h w r (j e)", r=8, w=8, h=2, j=BAND_TILES
             )
             for h in range(2):
-                nc.gpsimd.dma_start(
+                nc.sync.dma_start(
                     out=x_band[h:P:2, :, :].rearrange("q j e -> q (j e)"), in_=x_runs[h]
                 )
             o_bands[band] = o_band
@@ -100,14 +100,18 @@ def tile_swintransformerblock_pa_t_kernel(tc, x, o, out_w, out_b, ln1_g, ln1_b, 
         nc.vector.memset(rows[:], 0.0)
         nc.vector.tensor_copy(out=rows[0:1, :, :], in_=vectors[:])
         gain_ps = [const_ps.tile([P, BANK], F32, name="gain_ps%d" % h) for h in range(HALVES)]
-        shift_ps = [const_ps.tile([P, BANK], F32, name="shift_ps%d" % h) for h in range(HALVES)]
+        shift_ps = const_ps.tile([P, BANK], F32)
+        shift_sb = consts.tile([P, BANK], F32)
         bias_bc = consts.tile([P, E], BF16)
         for h in range(HALVES):
             nc.tensor.matmul(out=gain_ps[h][:], lhsT=ones[:], rhs=rows[:, 0, half(h)], start=True, stop=True)
-            nc.tensor.matmul(out=shift_ps[h][:], lhsT=ones[:], rhs=rows[:, 1, half(h)], start=True, stop=True)
             bias_ps = acc_ps.tile([P, BANK], F32, tag="acc%d" % h)
             nc.tensor.matmul(out=bias_ps[:], lhsT=ones[:], rhs=rows[:, 2, half(h)], start=True, stop=True)
             nc.scalar.copy(out=bias_bc[:, half(h)], in_=bias_ps[:])
+        nc.tensor.matmul(out=shift_ps[:], lhsT=ones[:], rhs=rows[:, 1, half(0)], start=True, stop=True)
+        shift_hi_ps = acc_ps.tile([P, BANK], F32, tag="acc0")
+        nc.tensor.matmul(out=shift_hi_ps[:], lhsT=ones[:], rhs=rows[:, 1, half(1)], start=True, stop=True)
+        nc.scalar.copy(out=shift_sb[:], in_=shift_hi_ps[:])
 
         w_words = w_raw[:].bitcast(F32)
         w_grouped = weights.tile([P, PASSES, E, PACK], BF16, align_bytes=64)
@@ -246,8 +250,8 @@ def tile_swintransformerblock_pa_t_kernel(tc, x, o, out_w, out_b, ln1_g, ln1_b, 
             y = normed[i]
             for h in range(HALVES):
                 nc.vector.tensor_tensor(out=y[:, half(h)], in0=y[:, half(h)], in1=gain_ps[h][:], op=ALU.mult)
-            for h in range(HALVES):
-                nc.vector.tensor_tensor(out=y[:, half(h)], in0=y[:, half(h)], in1=shift_ps[h][:], op=ALU.add)
+            nc.vector.tensor_tensor(out=y[:, half(0)], in0=y[:, half(0)], in1=shift_ps[:], op=ALU.add)
+            nc.gpsimd.tensor_tensor(out=y[:, half(1)], in0=y[:, half(1)], in1=shift_sb[:], op=ALU.add)
             tokens = slice(band * BAND_TOKENS, (band + 1) * BAND_TOKENS)
             nc.sync.dma_start(
                 out=out_tok[tokens, :].rearrange("(p j) e -> p j e", j=BAND_TILES)[:, j, :], in_=y[:]

@@ -49,7 +49,6 @@ def tile_swintransformerblock_pa_t_kernel(tc, x, o, out_w, out_b, ln1_g, ln1_b, 
         bands = ctx.enter_context(tc.tile_pool(name="bands", bufs=LOAD_LEAD))
         operands = ctx.enter_context(tc.tile_pool(name="operands", bufs=2))
         work = ctx.enter_context(tc.tile_pool(name="work", bufs=4))
-        biased = ctx.enter_context(tc.tile_pool(name="biased", bufs=BIAS_LEAD))
         small = ctx.enter_context(tc.tile_pool(name="small", bufs=4))
         const_ps = ctx.enter_context(tc.psum_pool(name="const_ps", bufs=1))
         acc_ps = ctx.enter_context(tc.psum_pool(name="acc_ps", bufs=1))
@@ -100,18 +99,14 @@ def tile_swintransformerblock_pa_t_kernel(tc, x, o, out_w, out_b, ln1_g, ln1_b, 
         nc.vector.memset(rows[:], 0.0)
         nc.vector.tensor_copy(out=rows[0:1, :, :], in_=vectors[:])
         gain_ps = [const_ps.tile([P, BANK], F32, name="gain_ps%d" % h) for h in range(HALVES)]
-        shift_ps = const_ps.tile([P, BANK], F32)
-        shift_sb = consts.tile([P, BANK], F32)
+        shift_ps = [const_ps.tile([P, BANK], F32, name="shift_ps%d" % h) for h in range(HALVES)]
         bias_bc = consts.tile([P, E], BF16)
         for h in range(HALVES):
             nc.tensor.matmul(out=gain_ps[h][:], lhsT=ones[:], rhs=rows[:, 0, half(h)], start=True, stop=True)
+            nc.tensor.matmul(out=shift_ps[h][:], lhsT=ones[:], rhs=rows[:, 1, half(h)], start=True, stop=True)
             bias_ps = acc_ps.tile([P, BANK], F32, tag="acc%d" % h)
             nc.tensor.matmul(out=bias_ps[:], lhsT=ones[:], rhs=rows[:, 2, half(h)], start=True, stop=True)
             nc.scalar.copy(out=bias_bc[:, half(h)], in_=bias_ps[:])
-        nc.tensor.matmul(out=shift_ps[:], lhsT=ones[:], rhs=rows[:, 1, half(0)], start=True, stop=True)
-        shift_hi_ps = acc_ps.tile([P, BANK], F32, tag="acc0")
-        nc.tensor.matmul(out=shift_hi_ps[:], lhsT=ones[:], rhs=rows[:, 1, half(1)], start=True, stop=True)
-        nc.scalar.copy(out=shift_sb[:], in_=shift_hi_ps[:])
 
         w_words = w_raw[:].bitcast(F32)
         w_grouped = weights.tile([P, PASSES, E, PACK], BF16, align_bytes=64)
@@ -143,8 +138,6 @@ def tile_swintransformerblock_pa_t_kernel(tc, x, o, out_w, out_b, ln1_g, ln1_b, 
         resid = {}
         neg_mean = {}
         rstd = {}
-        neg_mean_rstd = {}
-        normed = {}
 
         def transpose_tile(i):
             band, j = divmod(i, BAND_TILES)
@@ -178,7 +171,7 @@ def tile_swintransformerblock_pa_t_kernel(tc, x, o, out_w, out_b, ln1_g, ln1_b, 
 
         def add_bias(i):
             band, j = divmod(i, BAND_TILES)
-            xb = biased.tile([P, E], F32, tag="x_bias")
+            xb = work.tile([P, E], F32, tag="x_bias")
             nc.gpsimd.tensor_tensor(out=xb[:], in0=x_bands[band][:, j, :], in1=bias_bc[:], op=ALU.add)
             x_bias[i] = xb
 
@@ -202,83 +195,70 @@ def tile_swintransformerblock_pa_t_kernel(tc, x, o, out_w, out_b, ln1_g, ln1_b, 
 
         def residual_tile(i):
             r = work.tile([P, E], F32, tag="resid")
-            sums = small.tile([P, HALVES], F32, tag="sums")
             for h in range(HALVES):
-                nc.vector.scalar_tensor_tensor(
-                    out=r[:, half(h)],
-                    in0=acc[i][h][:],
-                    scalar=1.0,
-                    in1=x_bias[i][:, half(h)],
-                    op0=ALU.mult,
-                    op1=ALU.add,
-                    accum_out=sums[:, h : h + 1],
-                )
+                nc.vector.tensor_tensor(out=r[:, half(h)], in0=acc[i][h][:], in1=x_bias[i][:, half(h)], op=ALU.add)
             resid[i] = r
-            return sums
 
-        def mean_tile(i, sums):
-            scaled = small.tile([P, HALVES], F32, tag="scaled")
+        def mean_tile(i):
+            unread = work.tile([P, E], BF16, tag="unread_scaled")
             nm = small.tile([P, 1], F32, tag="neg_mean")
-            nc.scalar.activation(out=scaled[:], in_=sums[:], func=ACT.Identity, scale=-1.0 / E, accum_out=nm[:])
+            nc.scalar.activation(out=unread[:], in_=resid[i][:], func=ACT.Identity, scale=-1.0 / E, accum_out=nm[:])
             neg_mean[i] = nm
 
-        def squares_tile(i):
-            squares = work.tile([P, E], BF16, tag="squares")
+        def variance_tile(i):
+            unread = work.tile([P, E], BF16, tag="unread_squares")
             ssq = small.tile([P, 1], F32, tag="ssq")
             nc.scalar.activation(
-                out=squares[:], in_=resid[i][:], func=ACT.Square, bias=neg_mean[i][:], accum_out=ssq[:]
+                out=unread[:], in_=resid[i][:], func=ACT.Square, bias=neg_mean[i][:], accum_out=ssq[:]
             )
-            return ssq
-
-        def rstd_tile(i, ssq):
             rs = small.tile([P, 1], F32, tag="rstd")
             nc.scalar.activation(out=rs[:], in_=ssq[:], func=ACT.Abs_reciprocal_sqrt, bias=eps[:], scale=1.0 / E)
-            nb = small.tile([P, 1], F32, tag="neg_mean_rstd")
-            nc.scalar.activation(out=nb[:], in_=neg_mean[i][:], func=ACT.Copy, scale=rs[:])
             rstd[i] = rs
-            neg_mean_rstd[i] = nb
-
-        def normalise_tile(i):
-            y = work.tile([P, E], F32, tag="y")
-            nc.scalar.activation(
-                out=y[:], in_=resid[i][:], func=ACT.Identity, scale=rstd[i][:], bias=neg_mean_rstd[i][:]
-            )
-            normed[i] = y
 
         def affine_tile(i):
             band, j = divmod(i, BAND_TILES)
-            y = normed[i]
+            y = work.tile([P, E], F32, tag="y")
             for h in range(HALVES):
-                nc.vector.tensor_tensor(out=y[:, half(h)], in0=y[:, half(h)], in1=gain_ps[h][:], op=ALU.mult)
-            nc.vector.tensor_tensor(out=y[:, half(0)], in0=y[:, half(0)], in1=shift_ps[:], op=ALU.add)
-            nc.gpsimd.tensor_tensor(out=y[:, half(1)], in0=y[:, half(1)], in1=shift_sb[:], op=ALU.add)
+                nc.vector.scalar_tensor_tensor(
+                    out=y[:, half(h)],
+                    in0=resid[i][:, half(h)],
+                    scalar=neg_mean[i][:],
+                    in1=gain_ps[h][:],
+                    op0=ALU.add,
+                    op1=ALU.mult,
+                )
+            for h in range(HALVES):
+                nc.vector.scalar_tensor_tensor(
+                    out=y[:, half(h)],
+                    in0=y[:, half(h)],
+                    scalar=rstd[i][:],
+                    in1=shift_ps[h][:],
+                    op0=ALU.mult,
+                    op1=ALU.add,
+                )
             tokens = slice(band * BAND_TOKENS, (band + 1) * BAND_TOKENS)
             nc.sync.dma_start(
                 out=out_tok[tokens, :].rearrange("(p j) e -> p j e", j=BAND_TILES)[:, j, :], in_=y[:]
             )
 
-        for s in range(-TRANSPOSE_LEAD, N_TILES + 2):
+        for s in range(-TRANSPOSE_LEAD, N_TILES + 1):
             if s + TRANSPOSE_LEAD < N_TILES:
                 turned = transpose_tile(s + TRANSPOSE_LEAD)
             if 0 <= s + 1 < N_TILES and (s + 1) % BAND_TILES == 0:
                 quantise_band((s + 1) // BAND_TILES)
-            if 0 <= s < N_TILES:
-                sums = residual_tile(s)
             if 0 <= s + BIAS_LEAD < N_TILES:
                 add_bias(s + BIAS_LEAD)
+            if 0 <= s < N_TILES:
+                residual_tile(s)
             if 0 <= s + 1 < N_TILES:
                 matmul_tile(s + 1)
             if 0 <= s < N_TILES:
-                mean_tile(s, sums)
+                mean_tile(s)
             if s + TRANSPOSE_LEAD < N_TILES:
                 regroup_tile(s + TRANSPOSE_LEAD, turned)
             if 0 <= s < N_TILES:
-                ssq = squares_tile(s)
-            if 0 <= s - 1 < N_TILES:
-                normalise_tile(s - 1)
-            if 0 <= s < N_TILES:
-                rstd_tile(s, ssq)
-            if 0 <= s - 2:
-                affine_tile(s - 2)
+                variance_tile(s)
+            if 0 <= s - 1:
+                affine_tile(s - 1)
             if s >= 0 and s % BAND_TILES == 2 and s // BAND_TILES + LOAD_LEAD < N_BANDS:
                 load_band(s // BAND_TILES + LOAD_LEAD)

@@ -16,7 +16,6 @@ E = 1024
 N_TOKENS = 4096
 BAND_TOKENS = 512
 BAND_TILES = BAND_TOKENS // P
-N_BANDS = N_TOKENS // BAND_TOKENS
 N_TILES = N_TOKENS // P
 PACK = 4
 PASSES = E // (P * PACK)
@@ -24,11 +23,13 @@ WORD_BLOCKS = E // 2 // P
 BANK = 512
 HALVES = E // BANK
 C_TILES = E // P
+W_LOADS = 4
 LN_EPS = 1e-5
 
-TRANSPOSE_LEAD = 5
-BIAS_LEAD = 2
-LOAD_LEAD = 3
+TRANSPOSE_LEAD = 3
+QUANTISE_LEAD = 2
+BIAS_LEAD = 4
+LOAD_LEAD = 8
 
 FLOPS = 2 * N_TOKENS * E * E
 
@@ -43,11 +44,15 @@ def tile_swintransformerblock_pa_t_kernel(tc, x, o, out_w, out_b, ln1_g, ln1_b, 
     o_tok = o.rearrange("l n e -> (l n) e")
     out_tok = out.rearrange("l n e -> (l n) e")
 
+    def band_rows(i):
+        band = i // BAND_TILES
+        return slice(band * BAND_TOKENS, (band + 1) * BAND_TOKENS)
+
     with ExitStack() as ctx:
         consts = ctx.enter_context(tc.tile_pool(name="consts", bufs=1))
         weights = ctx.enter_context(tc.tile_pool(name="weights", bufs=1))
-        bands = ctx.enter_context(tc.tile_pool(name="bands", bufs=LOAD_LEAD))
-        operands = ctx.enter_context(tc.tile_pool(name="operands", bufs=2))
+        inputs = ctx.enter_context(tc.tile_pool(name="inputs", bufs=LOAD_LEAD))
+        operands = ctx.enter_context(tc.tile_pool(name="operands", bufs=3))
         work = ctx.enter_context(tc.tile_pool(name="work", bufs=4))
         small = ctx.enter_context(tc.tile_pool(name="small", bufs=4))
         const_ps = ctx.enter_context(tc.psum_pool(name="const_ps", bufs=1))
@@ -55,36 +60,32 @@ def tile_swintransformerblock_pa_t_kernel(tc, x, o, out_w, out_b, ln1_g, ln1_b, 
         turn_ps = ctx.enter_context(tc.psum_pool(name="turn_ps", bufs=2))
         ctx.enter_context(tc.manual_schedule())
 
-        o_bands = {}
-        x_bands = {}
+        o_tiles = {}
+        x_tiles = {}
 
-        def load_band(band):
-            tokens = slice(band * BAND_TOKENS, (band + 1) * BAND_TOKENS)
-            o_band = bands.tile([P, BAND_TILES, E], BF16, tag="o_band")
+        def load_tile(i):
+            j = i % BAND_TILES
+            o_tile = inputs.tile([P, E], BF16, tag="o_tile")
             nc.sync.dma_start(
-                out=o_band[:], in_=o_tok[tokens, :].rearrange("(p j) e -> p j e", j=BAND_TILES)
+                out=o_tile[:], in_=o_tok[band_rows(i), :].rearrange("(p j) e -> p j e", j=BAND_TILES)[:, j, :]
             )
-            x_band = bands.tile([P, BAND_TILES, E], BF16, tag="x_band")
-            x_runs = x_tok[tokens, :].rearrange(
-                "(r w h j) e -> h w r (j e)", r=8, w=8, h=2, j=BAND_TILES
-            )
+            x_tile = inputs.tile([P, E], BF16, tag="x_tile")
+            x_runs = x_tok[band_rows(i), :].rearrange("(r w h j) e -> h j w r e", r=8, w=8, h=2, j=BAND_TILES)
             for h in range(2):
-                nc.sync.dma_start(
-                    out=x_band[h:P:2, :, :].rearrange("q j e -> q (j e)"), in_=x_runs[h]
-                )
-            o_bands[band] = o_band
-            x_bands[band] = x_band
+                nc.sync.dma_start(out=x_tile[h:P:2, :], in_=x_runs[h, j])
+            o_tiles[i] = o_tile
+            x_tiles[i] = x_tile
 
         vectors = consts.tile([1, 3, E], BF16)
         for v, vec in enumerate((ln1_g, ln1_b, out_b)):
             nc.sync.dma_start(out=vectors[0:1, v, :], in_=vec.rearrange("(a e) -> a e", a=1))
         w_raw = weights.tile([P, C_TILES, E], BF16)
         w_view = out_w.rearrange("(c p) k -> p c k", p=P)
-        for h in range(HALVES):
-            blocks = slice(h * C_TILES // HALVES, (h + 1) * C_TILES // HALVES)
+        for q in range(W_LOADS):
+            blocks = slice(q * C_TILES // W_LOADS, (q + 1) * C_TILES // W_LOADS)
             nc.sync.dma_start(out=w_raw[:, blocks, :], in_=w_view[:, blocks, :])
-        for band in range(LOAD_LEAD):
-            load_band(band)
+        for i in range(LOAD_LEAD):
+            load_tile(i)
 
         ident = consts.tile([P, P], F32)
         make_identity(nc, ident[:])
@@ -130,7 +131,6 @@ def tile_swintransformerblock_pa_t_kernel(tc, x, o, out_w, out_b, ln1_g, ln1_b, 
                     in_=w_grouped[:, g, half(h), :].rearrange("p c f -> p (c f)"),
                 )
 
-        grouped = {}
         o_codes = {}
         o_scales = {}
         x_bias = {}
@@ -140,52 +140,41 @@ def tile_swintransformerblock_pa_t_kernel(tc, x, o, out_w, out_b, ln1_g, ln1_b, 
         rstd = {}
 
         def transpose_tile(i):
-            band, j = divmod(i, BAND_TILES)
-            if j == 0:
-                grouped[band] = operands.tile(
-                    [P, BAND_TILES, PASSES, P, PACK], BF16, tag="grouped", name="grouped", align_bytes=64
-                )
             turned = turn_ps.tile([P, WORD_BLOCKS, P], F32, tag="turned")
-            o_words = o_bands[band][:].bitcast(F32)
+            o_words = o_tiles[i][:].bitcast(F32)
             for b in range(WORD_BLOCKS):
-                nc.tensor.transpose(turned[:, b, :], o_words[:, j, b * P : (b + 1) * P], ident[:])
+                nc.tensor.transpose(turned[:, b, :], o_words[:, b * P : (b + 1) * P], ident[:])
             return turned
 
-        def regroup_tile(i, turned):
-            band, j = divmod(i, BAND_TILES)
-            nc.scalar.copy(
-                out=grouped[band][:].bitcast(F32)[:, j],
-                in_=turned[:].rearrange("p (g u) t -> p g t u", u=2),
-            )
+        def regroup_tile(turned):
+            grouped = operands.tile([P, PASSES, P, PACK], BF16, tag="grouped", align_bytes=64)
+            nc.scalar.copy(out=grouped[:].bitcast(F32), in_=turned[:].rearrange("p (g u) t -> p g t u", u=2))
+            return grouped
 
-        def quantise_band(band):
-            codes = operands.tile([P, BAND_TILES * PASSES * P], U32, tag="codes", align_bytes=64)
-            scales = operands.tile([P, BAND_TILES * PASSES * P], U8, tag="scales", align_bytes=64)
+        def quantise_tile(i, grouped):
+            codes = operands.tile([P, PASSES * P], U32, tag="codes", align_bytes=64)
+            scales = operands.tile([P, PASSES * P], U8, tag="scales", align_bytes=64)
             nc.vector.quantize_mx(
-                out=codes[:].bitcast(FP8X4),
-                scales=scales[:],
-                in_=grouped[band][:].rearrange("p j g t f -> p (j g t f)"),
+                out=codes[:].bitcast(FP8X4), scales=scales[:], in_=grouped[:].rearrange("p g t f -> p (g t f)")
             )
-            o_codes[band] = codes
-            o_scales[band] = scales
+            o_codes[i] = codes
+            o_scales[i] = scales
 
         def add_bias(i):
-            band, j = divmod(i, BAND_TILES)
             xb = work.tile([P, E], F32, tag="x_bias")
-            nc.gpsimd.tensor_tensor(out=xb[:], in0=x_bands[band][:, j, :], in1=bias_bc[:], op=ALU.add)
+            nc.gpsimd.tensor_tensor(out=xb[:], in0=x_tiles[i][:], in1=bias_bc[:], op=ALU.add)
             x_bias[i] = xb
 
         def matmul_tile(i):
-            band, j = divmod(i, BAND_TILES)
             acc[i] = []
             for h in range(HALVES):
                 bank = acc_ps.tile([P, BANK], F32, tag="acc%d" % h)
                 for g in range(PASSES):
-                    cols = slice((j * PASSES + g) * P, (j * PASSES + g + 1) * P)
+                    cols = slice(g * P, (g + 1) * P)
                     nc.tensor.matmul_mx(
                         out=bank[:],
-                        lhsT=o_codes[band][:, cols].bitcast(FP8X4),
-                        lhsT_scale=o_scales[band][:, cols],
+                        lhsT=o_codes[i][:, cols].bitcast(FP8X4),
+                        lhsT_scale=o_scales[i][:, cols],
                         rhs=w_codes[:, g, half(h)].bitcast(FP8X4),
                         rhs_scale=w_scales[:, g, half(h)],
                         start=(g == 0),
@@ -193,11 +182,12 @@ def tile_swintransformerblock_pa_t_kernel(tc, x, o, out_w, out_b, ln1_g, ln1_b, 
                     )
                 acc[i].append(bank)
 
-        def residual_tile(i):
-            r = work.tile([P, E], F32, tag="resid")
-            for h in range(HALVES):
-                nc.vector.tensor_tensor(out=r[:, half(h)], in0=acc[i][h][:], in1=x_bias[i][:, half(h)], op=ALU.add)
-            resid[i] = r
+        def residual_half(i, h):
+            if h == 0:
+                resid[i] = work.tile([P, E], F32, tag="resid", name="resid")
+            nc.vector.tensor_tensor(
+                out=resid[i][:, half(h)], in0=acc[i][h][:], in1=x_bias[i][:, half(h)], op=ALU.add
+            )
 
         def mean_tile(i):
             unread = work.tile([P, E], BF16, tag="unread_scaled")
@@ -216,7 +206,6 @@ def tile_swintransformerblock_pa_t_kernel(tc, x, o, out_w, out_b, ln1_g, ln1_b, 
             rstd[i] = rs
 
         def affine_tile(i):
-            band, j = divmod(i, BAND_TILES)
             y = work.tile([P, E], F32, tag="y")
             for h in range(HALVES):
                 nc.vector.scalar_tensor_tensor(
@@ -236,29 +225,35 @@ def tile_swintransformerblock_pa_t_kernel(tc, x, o, out_w, out_b, ln1_g, ln1_b, 
                     op0=ALU.mult,
                     op1=ALU.add,
                 )
-            tokens = slice(band * BAND_TOKENS, (band + 1) * BAND_TOKENS)
             nc.sync.dma_start(
-                out=out_tok[tokens, :].rearrange("(p j) e -> p j e", j=BAND_TILES)[:, j, :], in_=y[:]
+                out=out_tok[band_rows(i), :].rearrange("(p j) e -> p j e", j=BAND_TILES)[:, i % BAND_TILES, :],
+                in_=y[:],
             )
 
-        for s in range(-TRANSPOSE_LEAD, N_TILES + 1):
-            if s + TRANSPOSE_LEAD < N_TILES:
+        def is_tile(i):
+            return 0 <= i < N_TILES
+
+        grouped_tiles = {}
+        for s in range(-max(TRANSPOSE_LEAD, BIAS_LEAD), N_TILES + 1):
+            if is_tile(s + TRANSPOSE_LEAD):
                 turned = transpose_tile(s + TRANSPOSE_LEAD)
-            if 0 <= s + 1 < N_TILES and (s + 1) % BAND_TILES == 0:
-                quantise_band((s + 1) // BAND_TILES)
-            if 0 <= s + BIAS_LEAD < N_TILES:
+            if is_tile(s):
+                residual_half(s, 0)
+            if is_tile(s + QUANTISE_LEAD):
+                quantise_tile(s + QUANTISE_LEAD, grouped_tiles[s + QUANTISE_LEAD])
+            if is_tile(s):
+                residual_half(s, 1)
+            if is_tile(s + BIAS_LEAD):
                 add_bias(s + BIAS_LEAD)
-            if 0 <= s < N_TILES:
-                residual_tile(s)
-            if 0 <= s + 1 < N_TILES:
+            if is_tile(s + 1):
                 matmul_tile(s + 1)
-            if 0 <= s < N_TILES:
+            if is_tile(s):
                 mean_tile(s)
-            if s + TRANSPOSE_LEAD < N_TILES:
-                regroup_tile(s + TRANSPOSE_LEAD, turned)
-            if 0 <= s < N_TILES:
+            if is_tile(s + TRANSPOSE_LEAD):
+                grouped_tiles[s + TRANSPOSE_LEAD] = regroup_tile(turned)
+            if is_tile(s):
                 variance_tile(s)
-            if 0 <= s - 1:
+            if is_tile(s - 1):
                 affine_tile(s - 1)
-            if s >= 0 and s % BAND_TILES == 2 and s // BAND_TILES + LOAD_LEAD < N_BANDS:
-                load_band(s // BAND_TILES + LOAD_LEAD)
+            if s >= 0 and is_tile(s + LOAD_LEAD):
+                load_tile(s + LOAD_LEAD)

@@ -23,8 +23,11 @@ WORD_BLOCKS = E // 2 // P
 BANK = 512
 HALVES = E // BANK
 C_TILES = E // P
-W_LOADS = 4
+W_GROUP = 2
 LN_EPS = 1e-5
+BIAS = 0
+GAIN = 1
+SHIFT = 2
 
 TRANSPOSE_LEAD = 3
 QUANTISE_LEAD = 2
@@ -77,13 +80,12 @@ def tile_swintransformerblock_pa_t_kernel(tc, x, o, out_w, out_b, ln1_g, ln1_b, 
             x_tiles[i] = x_tile
 
         vectors = consts.tile([1, 3, E], BF16)
-        for v, vec in enumerate((ln1_g, ln1_b, out_b)):
+        for v, vec in enumerate((out_b, ln1_g, ln1_b)):
             nc.sync.dma_start(out=vectors[0:1, v, :], in_=vec.rearrange("(a e) -> a e", a=1))
         w_raw = weights.tile([P, C_TILES, E], BF16)
         w_view = out_w.rearrange("(c p) k -> p c k", p=P)
-        for q in range(W_LOADS):
-            blocks = slice(q * C_TILES // W_LOADS, (q + 1) * C_TILES // W_LOADS)
-            nc.sync.dma_start(out=w_raw[:, blocks, :], in_=w_view[:, blocks, :])
+        for c in range(C_TILES):
+            nc.sync.dma_start(out=w_raw[:, c, :], in_=w_view[:, c, :])
         for i in range(LOAD_LEAD):
             load_tile(i)
 
@@ -97,25 +99,18 @@ def tile_swintransformerblock_pa_t_kernel(tc, x, o, out_w, out_b, ln1_g, ln1_b, 
         nc.scalar.activation(out=warm[:], in_=eps[:], func=ACT.Abs_reciprocal_sqrt)
 
         rows = consts.tile([P, 3, E], BF16)
-        nc.vector.memset(rows[:], 0.0)
-        nc.vector.tensor_copy(out=rows[0:1, :, :], in_=vectors[:])
-        gain_ps = [const_ps.tile([P, BANK], F32, name="gain_ps%d" % h) for h in range(HALVES)]
-        shift_ps = [const_ps.tile([P, BANK], F32, name="shift_ps%d" % h) for h in range(HALVES)]
-        bias_bc = consts.tile([P, E], BF16)
-        for h in range(HALVES):
-            nc.tensor.matmul(out=gain_ps[h][:], lhsT=ones[:], rhs=rows[:, 0, half(h)], start=True, stop=True)
-            nc.tensor.matmul(out=shift_ps[h][:], lhsT=ones[:], rhs=rows[:, 1, half(h)], start=True, stop=True)
-            bias_ps = acc_ps.tile([P, BANK], F32, tag="acc%d" % h)
-            nc.tensor.matmul(out=bias_ps[:], lhsT=ones[:], rhs=rows[:, 2, half(h)], start=True, stop=True)
-            nc.scalar.copy(out=bias_bc[:, half(h)], in_=bias_ps[:])
+        for v in (BIAS, GAIN, SHIFT):
+            nc.vector.memset(rows[:, v, :], 0.0)
+            nc.vector.tensor_copy(out=rows[0:1, v, :], in_=vectors[0:1, v, :])
 
         w_words = w_raw[:].bitcast(F32)
         w_grouped = weights.tile([P, PASSES, E, PACK], BF16, align_bytes=64)
         w_grouped_words = w_grouped[:].bitcast(F32)
         w_codes = weights.tile([P, PASSES, E], U32, align_bytes=64)
         w_scales = weights.tile([P, PASSES, E], U8, align_bytes=64)
-        for h in range(HALVES):
-            for c in range(h * C_TILES // HALVES, (h + 1) * C_TILES // HALVES):
+
+        def prepare_weights(first):
+            for c in range(first, first + W_GROUP):
                 turned = turn_ps.tile([P, WORD_BLOCKS, P], F32, tag="turned")
                 for b in range(WORD_BLOCKS):
                     nc.tensor.transpose(turned[:, b, :], w_words[:, c, b * P : (b + 1) * P], ident[:])
@@ -124,13 +119,25 @@ def tile_swintransformerblock_pa_t_kernel(tc, x, o, out_w, out_b, ln1_g, ln1_b, 
                     out=w_grouped_words[:, :, c * P : (c + 1) * P, :],
                     in_=turned[:].rearrange("p (g u) c -> p g c u", u=2),
                 )
+            channels = slice(first * P, (first + W_GROUP) * P)
             for g in range(PASSES):
                 nc.vector.quantize_mx(
-                    out=w_codes[:, g, half(h)].bitcast(FP8X4),
-                    scales=w_scales[:, g, half(h)],
-                    in_=w_grouped[:, g, half(h), :].rearrange("p c f -> p (c f)"),
+                    out=w_codes[:, g, channels].bitcast(FP8X4),
+                    scales=w_scales[:, g, channels],
+                    in_=w_grouped[:, g, channels, :].rearrange("p c f -> p (c f)"),
                 )
 
+        prepare_weights(0)
+        bias_bc = consts.tile([P, E], BF16)
+        for h in range(HALVES):
+            bias_ps = acc_ps.tile([P, BANK], F32, tag="acc%d" % h)
+            nc.tensor.matmul(out=bias_ps[:], lhsT=ones[:], rhs=rows[:, BIAS, half(h)], start=True, stop=True)
+            nc.scalar.copy(out=bias_bc[:, half(h)], in_=bias_ps[:])
+        for first in range(W_GROUP, C_TILES, W_GROUP):
+            prepare_weights(first)
+
+        gain_ps = [const_ps.tile([P, BANK], F32, name="gain_ps%d" % h) for h in range(HALVES)]
+        shift_ps = [const_ps.tile([P, BANK], F32, name="shift_ps%d" % h) for h in range(HALVES)]
         o_codes = {}
         o_scales = {}
         x_bias = {}
@@ -216,6 +223,7 @@ def tile_swintransformerblock_pa_t_kernel(tc, x, o, out_w, out_b, ln1_g, ln1_b, 
                     op0=ALU.add,
                     op1=ALU.mult,
                 )
+            out_rows = out_tok[band_rows(i), :].rearrange("(p j) e -> p j e", j=BAND_TILES)[:, i % BAND_TILES, :]
             for h in range(HALVES):
                 nc.vector.scalar_tensor_tensor(
                     out=y[:, half(h)],
@@ -225,18 +233,17 @@ def tile_swintransformerblock_pa_t_kernel(tc, x, o, out_w, out_b, ln1_g, ln1_b, 
                     op0=ALU.mult,
                     op1=ALU.add,
                 )
-            nc.sync.dma_start(
-                out=out_tok[band_rows(i), :].rearrange("(p j) e -> p j e", j=BAND_TILES)[:, i % BAND_TILES, :],
-                in_=y[:],
-            )
+                nc.sync.dma_start(out=out_rows[:, half(h)], in_=y[:, half(h)])
 
         def is_tile(i):
             return 0 <= i < N_TILES
 
         grouped_tiles = {}
-        for s in range(-max(TRANSPOSE_LEAD, BIAS_LEAD), N_TILES + 1):
+        turned_tiles = {}
+
+        def step(s):
             if is_tile(s + TRANSPOSE_LEAD):
-                turned = transpose_tile(s + TRANSPOSE_LEAD)
+                turned_tiles[s + TRANSPOSE_LEAD] = transpose_tile(s + TRANSPOSE_LEAD)
             if is_tile(s):
                 residual_half(s, 0)
             if is_tile(s + QUANTISE_LEAD):
@@ -250,10 +257,18 @@ def tile_swintransformerblock_pa_t_kernel(tc, x, o, out_w, out_b, ln1_g, ln1_b, 
             if is_tile(s):
                 mean_tile(s)
             if is_tile(s + TRANSPOSE_LEAD):
-                grouped_tiles[s + TRANSPOSE_LEAD] = regroup_tile(turned)
+                grouped_tiles[s + TRANSPOSE_LEAD] = regroup_tile(turned_tiles[s + TRANSPOSE_LEAD])
             if is_tile(s):
                 variance_tile(s)
             if is_tile(s - 1):
                 affine_tile(s - 1)
             if s >= 0 and is_tile(s + LOAD_LEAD):
                 load_tile(s + LOAD_LEAD)
+
+        for s in range(-max(TRANSPOSE_LEAD, BIAS_LEAD), 0):
+            step(s)
+        for h in range(HALVES):
+            nc.tensor.matmul(out=gain_ps[h][:], lhsT=ones[:], rhs=rows[:, GAIN, half(h)], start=True, stop=True)
+            nc.tensor.matmul(out=shift_ps[h][:], lhsT=ones[:], rhs=rows[:, SHIFT, half(h)], start=True, stop=True)
+        for s in range(0, N_TILES + 1):
+            step(s)

@@ -31,7 +31,7 @@ SHIFT = 2
 
 TRANSPOSE_LEAD = 3
 QUANTISE_LEAD = 2
-BIAS_LEAD = 4
+BIAS_LEAD = 2
 LOAD_LEAD = 8
 
 FLOPS = 2 * N_TOKENS * E * E
@@ -168,8 +168,9 @@ def tile_swintransformerblock_pa_t_kernel(tc, x, o, out_w, out_b, ln1_g, ln1_b, 
             o_scales[i] = scales
 
         def add_bias(i):
-            xb = work.tile([P, E], F32, tag="x_bias")
-            nc.gpsimd.tensor_tensor(out=xb[:], in0=x_tiles[i][:], in1=bias_bc[:], op=ALU.add)
+            engine = nc.vector if i < BIAS_LEAD else nc.gpsimd
+            xb = work.tile([P, E], F32, tag="x_bias", bufs=BIAS_LEAD)
+            engine.tensor_tensor(out=xb[:], in0=x_tiles[i][:], in1=bias_bc[:], op=ALU.add)
             x_bias[i] = xb
 
         def matmul_tile(i):

@@ -29,8 +29,10 @@ BIAS = 0
 GAIN = 1
 SHIFT = 2
 
-TRANSPOSE_LEAD = 3
+FIRST_TRANSPOSE_LEAD = 3
+TRANSPOSE_LEAD = 5
 QUANTISE_LEAD = 2
+BAND_QUANTISE_LEAD = 1
 BIAS_LEAD = 2
 LOAD_LEAD = 8
 
@@ -55,7 +57,7 @@ def tile_swintransformerblock_pa_t_kernel(tc, x, o, out_w, out_b, ln1_g, ln1_b, 
         consts = ctx.enter_context(tc.tile_pool(name="consts", bufs=1))
         weights = ctx.enter_context(tc.tile_pool(name="weights", bufs=1))
         inputs = ctx.enter_context(tc.tile_pool(name="inputs", bufs=LOAD_LEAD))
-        operands = ctx.enter_context(tc.tile_pool(name="operands", bufs=3))
+        operands = ctx.enter_context(tc.tile_pool(name="operands", bufs=2))
         work = ctx.enter_context(tc.tile_pool(name="work", bufs=4))
         small = ctx.enter_context(tc.tile_pool(name="small", bufs=4))
         const_ps = ctx.enter_context(tc.psum_pool(name="const_ps", bufs=1))
@@ -138,6 +140,7 @@ def tile_swintransformerblock_pa_t_kernel(tc, x, o, out_w, out_b, ln1_g, ln1_b, 
 
         gain_ps = [const_ps.tile([P, BANK], F32, name="gain_ps%d" % h) for h in range(HALVES)]
         shift_ps = [const_ps.tile([P, BANK], F32, name="shift_ps%d" % h) for h in range(HALVES)]
+        grouped_bands = {}
         o_codes = {}
         o_scales = {}
         x_bias = {}
@@ -153,19 +156,27 @@ def tile_swintransformerblock_pa_t_kernel(tc, x, o, out_w, out_b, ln1_g, ln1_b, 
                 nc.tensor.transpose(turned[:, b, :], o_words[:, b * P : (b + 1) * P], ident[:])
             return turned
 
-        def regroup_tile(turned):
-            grouped = operands.tile([P, PASSES, P, PACK], BF16, tag="grouped", align_bytes=64)
-            nc.scalar.copy(out=grouped[:].bitcast(F32), in_=turned[:].rearrange("p (g u) t -> p g t u", u=2))
-            return grouped
-
-        def quantise_tile(i, grouped):
-            codes = operands.tile([P, PASSES * P], U32, tag="codes", align_bytes=64)
-            scales = operands.tile([P, PASSES * P], U8, tag="scales", align_bytes=64)
-            nc.vector.quantize_mx(
-                out=codes[:].bitcast(FP8X4), scales=scales[:], in_=grouped[:].rearrange("p g t f -> p (g t f)")
+        def regroup_tile(i, turned):
+            band, j = divmod(i, BAND_TILES)
+            if j == 0:
+                grouped_bands[band] = operands.tile(
+                    [P, BAND_TILES, PASSES, P, PACK], BF16, tag="grouped", name="grouped", align_bytes=64
+                )
+            nc.scalar.copy(
+                out=grouped_bands[band][:, j, :, :, :].bitcast(F32), in_=turned[:].rearrange("p (g u) t -> p g t u", u=2)
             )
-            o_codes[i] = codes
-            o_scales[i] = scales
+
+        def quantise_tiles(first, count):
+            band, j = divmod(first, BAND_TILES)
+            if j == 0:
+                o_codes[band] = operands.tile([P, BAND_TILES * PASSES * P], U32, tag="codes", name="codes", align_bytes=64)
+                o_scales[band] = operands.tile([P, BAND_TILES * PASSES * P], U8, tag="scales", name="scales", align_bytes=64)
+            cols = slice(j * PASSES * P, (j + count) * PASSES * P)
+            nc.vector.quantize_mx(
+                out=o_codes[band][:, cols].bitcast(FP8X4),
+                scales=o_scales[band][:, cols],
+                in_=grouped_bands[band][:, j : j + count, :, :, :].rearrange("p j g t f -> p (j g t f)"),
+            )
 
         def add_bias(i):
             engine = nc.vector if i < BIAS_LEAD else nc.gpsimd
@@ -178,11 +189,12 @@ def tile_swintransformerblock_pa_t_kernel(tc, x, o, out_w, out_b, ln1_g, ln1_b, 
             for h in range(HALVES):
                 bank = acc_ps.tile([P, BANK], F32, tag="acc%d" % h)
                 for g in range(PASSES):
-                    cols = slice(g * P, (g + 1) * P)
+                    block = (i % BAND_TILES) * PASSES + g
+                    cols = slice(block * P, (block + 1) * P)
                     nc.tensor.matmul_mx(
                         out=bank[:],
-                        lhsT=o_codes[i][:, cols].bitcast(FP8X4),
-                        lhsT_scale=o_scales[i][:, cols],
+                        lhsT=o_codes[i // BAND_TILES][:, cols].bitcast(FP8X4),
+                        lhsT_scale=o_scales[i // BAND_TILES][:, cols],
                         rhs=w_codes[:, g, half(h)].bitcast(FP8X4),
                         rhs_scale=w_scales[:, g, half(h)],
                         start=(g == 0),
@@ -239,16 +251,21 @@ def tile_swintransformerblock_pa_t_kernel(tc, x, o, out_w, out_b, ln1_g, ln1_b, 
         def is_tile(i):
             return 0 <= i < N_TILES
 
-        grouped_tiles = {}
         turned_tiles = {}
 
+        def first_to_turn(s):
+            return s + FIRST_TRANSPOSE_LEAD + min(max(s, 0), TRANSPOSE_LEAD - FIRST_TRANSPOSE_LEAD)
+
         def step(s):
-            if is_tile(s + TRANSPOSE_LEAD):
-                turned_tiles[s + TRANSPOSE_LEAD] = transpose_tile(s + TRANSPOSE_LEAD)
+            to_turn = [i for i in range(first_to_turn(s), first_to_turn(s + 1)) if is_tile(i)]
+            for i in to_turn:
+                turned_tiles[i] = transpose_tile(i)
             if is_tile(s):
                 residual_half(s, 0)
-            if is_tile(s + QUANTISE_LEAD):
-                quantise_tile(s + QUANTISE_LEAD, grouped_tiles[s + QUANTISE_LEAD])
+            if 0 <= s + QUANTISE_LEAD < BAND_TILES:
+                quantise_tiles(s + QUANTISE_LEAD, 1)
+            elif is_tile(s + BAND_QUANTISE_LEAD) and (s + BAND_QUANTISE_LEAD) % BAND_TILES == 0:
+                quantise_tiles(s + BAND_QUANTISE_LEAD, BAND_TILES)
             if is_tile(s):
                 residual_half(s, 1)
             if is_tile(s + BIAS_LEAD):
@@ -257,8 +274,8 @@ def tile_swintransformerblock_pa_t_kernel(tc, x, o, out_w, out_b, ln1_g, ln1_b, 
                 matmul_tile(s + 1)
             if is_tile(s):
                 mean_tile(s)
-            if is_tile(s + TRANSPOSE_LEAD):
-                grouped_tiles[s + TRANSPOSE_LEAD] = regroup_tile(turned_tiles[s + TRANSPOSE_LEAD])
+            for i in to_turn:
+                regroup_tile(i, turned_tiles[i])
             if is_tile(s):
                 variance_tile(s)
             if is_tile(s - 1):
@@ -266,7 +283,7 @@ def tile_swintransformerblock_pa_t_kernel(tc, x, o, out_w, out_b, ln1_g, ln1_b, 
             if s >= 0 and is_tile(s + LOAD_LEAD):
                 load_tile(s + LOAD_LEAD)
 
-        for s in range(-max(TRANSPOSE_LEAD, BIAS_LEAD), 0):
+        for s in range(-max(FIRST_TRANSPOSE_LEAD, BIAS_LEAD), 0):
             step(s)
         for h in range(HALVES):
             nc.tensor.matmul(out=gain_ps[h][:], lhsT=ones[:], rhs=rows[:, GAIN, half(h)], start=True, stop=True)

@@ -34,6 +34,7 @@ TRANSPOSE_LEAD = 5
 QUANTISE_LEAD = 2
 BAND_QUANTISE_LEAD = 1
 BIAS_LEAD = 2
+SHARED_TILE = 2
 LOAD_LEAD = 8
 
 FLOPS = 2 * N_TOKENS * E * E
@@ -140,6 +141,9 @@ def tile_swintransformerblock_pa_t_kernel(tc, x, o, out_w, out_b, ln1_g, ln1_b, 
 
         gain_ps = [const_ps.tile([P, BANK], F32, name="gain_ps%d" % h) for h in range(HALVES)]
         shift_ps = [const_ps.tile([P, BANK], F32, name="shift_ps%d" % h) for h in range(HALVES)]
+        shift_bc = consts.tile([P, BANK], BF16)
+        gained = {}
+        scaled = {}
         grouped_bands = {}
         o_codes = {}
         o_scales = {}
@@ -225,8 +229,12 @@ def tile_swintransformerblock_pa_t_kernel(tc, x, o, out_w, out_b, ln1_g, ln1_b, 
             nc.scalar.activation(out=rs[:], in_=ssq[:], func=ACT.Abs_reciprocal_sqrt, bias=eps[:], scale=1.0 / E)
             rstd[i] = rs
 
-        def affine_tile(i):
+        def is_shared(i):
+            return i % BAND_TILES == SHARED_TILE
+
+        def gain_tile(i):
             y = work.tile([P, E], F32, tag="y")
+            gained[i] = y
             for h in range(HALVES):
                 nc.vector.scalar_tensor_tensor(
                     out=y[:, half(h)],
@@ -236,16 +244,27 @@ def tile_swintransformerblock_pa_t_kernel(tc, x, o, out_w, out_b, ln1_g, ln1_b, 
                     op0=ALU.add,
                     op1=ALU.mult,
                 )
+
+        def scale_half(i):
+            sc = work.tile([P, BANK], F32, tag="scaled", bufs=2)
+            nc.scalar.activation(out=sc[:], in_=gained[i][:, half(1)], func=ACT.Identity, scale=rstd[i][:])
+            scaled[i] = sc
+
+        def shift_tile(i):
+            y = gained[i]
             out_rows = out_tok[band_rows(i), :].rearrange("(p j) e -> p j e", j=BAND_TILES)[:, i % BAND_TILES, :]
             for h in range(HALVES):
-                nc.vector.scalar_tensor_tensor(
-                    out=y[:, half(h)],
-                    in0=y[:, half(h)],
-                    scalar=rstd[i][:],
-                    in1=shift_ps[h][:],
-                    op0=ALU.mult,
-                    op1=ALU.add,
-                )
+                if h == 1 and is_shared(i):
+                    nc.gpsimd.tensor_tensor(out=y[:, half(h)], in0=scaled[i][:], in1=shift_bc[:], op=ALU.add)
+                else:
+                    nc.vector.scalar_tensor_tensor(
+                        out=y[:, half(h)],
+                        in0=y[:, half(h)],
+                        scalar=rstd[i][:],
+                        in1=shift_ps[h][:],
+                        op0=ALU.mult,
+                        op1=ALU.add,
+                    )
                 nc.sync.dma_start(out=out_rows[:, half(h)], in_=y[:, half(h)])
 
         def is_tile(i):
@@ -274,12 +293,16 @@ def tile_swintransformerblock_pa_t_kernel(tc, x, o, out_w, out_b, ln1_g, ln1_b, 
                 matmul_tile(s + 1)
             if is_tile(s):
                 mean_tile(s)
+            if is_tile(s - 1):
+                gain_tile(s - 1)
+                if is_shared(s - 1):
+                    scale_half(s - 1)
             for i in to_turn:
                 regroup_tile(i, turned_tiles[i])
             if is_tile(s):
                 variance_tile(s)
             if is_tile(s - 1):
-                affine_tile(s - 1)
+                shift_tile(s - 1)
             if s >= 0 and is_tile(s + LOAD_LEAD):
                 load_tile(s + LOAD_LEAD)
 
@@ -288,5 +311,6 @@ def tile_swintransformerblock_pa_t_kernel(tc, x, o, out_w, out_b, ln1_g, ln1_b, 
         for h in range(HALVES):
             nc.tensor.matmul(out=gain_ps[h][:], lhsT=ones[:], rhs=rows[:, GAIN, half(h)], start=True, stop=True)
             nc.tensor.matmul(out=shift_ps[h][:], lhsT=ones[:], rhs=rows[:, SHIFT, half(h)], start=True, stop=True)
+        nc.scalar.copy(out=shift_bc[:], in_=shift_ps[1][:])
         for s in range(0, N_TILES + 1):
             step(s)

@@ -34,7 +34,7 @@ TRANSPOSE_LEAD = 5
 QUANTISE_LEAD = 2
 BAND_QUANTISE_LEAD = 1
 BIAS_LEAD = 2
-SHARED_TILE = 2
+SHARED_TILE = 1
 LOAD_LEAD = 8
 
 FLOPS = 2 * N_TOKENS * E * E
@@ -62,7 +62,7 @@ def tile_swintransformerblock_pa_t_kernel(tc, x, o, out_w, out_b, ln1_g, ln1_b, 
         work = ctx.enter_context(tc.tile_pool(name="work", bufs=4))
         small = ctx.enter_context(tc.tile_pool(name="small", bufs=4))
         const_ps = ctx.enter_context(tc.psum_pool(name="const_ps", bufs=1))
-        acc_ps = ctx.enter_context(tc.psum_pool(name="acc_ps", bufs=1))
+        acc_ps = ctx.enter_context(tc.psum_pool(name="acc_ps", bufs=2))
         turn_ps = ctx.enter_context(tc.psum_pool(name="turn_ps", bufs=2))
         ctx.enter_context(tc.manual_schedule())
 
@@ -139,8 +139,8 @@ def tile_swintransformerblock_pa_t_kernel(tc, x, o, out_w, out_b, ln1_g, ln1_b, 
         for first in range(W_GROUP, C_TILES, W_GROUP):
             prepare_weights(first)
 
-        gain_ps = [const_ps.tile([P, BANK], F32, name="gain_ps%d" % h) for h in range(HALVES)]
-        shift_ps = [const_ps.tile([P, BANK], F32, name="shift_ps%d" % h) for h in range(HALVES)]
+        gain_ps = const_ps.tile([P, E], BF16, name="gain_ps")
+        shift_ps = const_ps.tile([P, E], BF16, name="shift_ps")
         shift_bc = consts.tile([P, BANK], BF16)
         gained = {}
         scaled = {}
@@ -235,15 +235,9 @@ def tile_swintransformerblock_pa_t_kernel(tc, x, o, out_w, out_b, ln1_g, ln1_b, 
         def gain_tile(i):
             y = work.tile([P, E], F32, tag="y")
             gained[i] = y
-            for h in range(HALVES):
-                nc.vector.scalar_tensor_tensor(
-                    out=y[:, half(h)],
-                    in0=resid[i][:, half(h)],
-                    scalar=neg_mean[i][:],
-                    in1=gain_ps[h][:],
-                    op0=ALU.add,
-                    op1=ALU.mult,
-                )
+            nc.vector.scalar_tensor_tensor(
+                out=y[:], in0=resid[i][:], scalar=neg_mean[i][:], in1=gain_ps[:], op0=ALU.add, op1=ALU.mult
+            )
 
         def scale_half(i):
             sc = work.tile([P, BANK], F32, tag="scaled", bufs=2)
@@ -253,19 +247,19 @@ def tile_swintransformerblock_pa_t_kernel(tc, x, o, out_w, out_b, ln1_g, ln1_b, 
         def shift_tile(i):
             y = gained[i]
             out_rows = out_tok[band_rows(i), :].rearrange("(p j) e -> p j e", j=BAND_TILES)[:, i % BAND_TILES, :]
-            for h in range(HALVES):
-                if h == 1 and is_shared(i):
-                    nc.gpsimd.tensor_tensor(out=y[:, half(h)], in0=scaled[i][:], in1=shift_bc[:], op=ALU.add)
-                else:
-                    nc.vector.scalar_tensor_tensor(
-                        out=y[:, half(h)],
-                        in0=y[:, half(h)],
-                        scalar=rstd[i][:],
-                        in1=shift_ps[h][:],
-                        op0=ALU.mult,
-                        op1=ALU.add,
-                    )
-                nc.sync.dma_start(out=out_rows[:, half(h)], in_=y[:, half(h)])
+            on_vector = half(0) if is_shared(i) else slice(0, E)
+            nc.vector.scalar_tensor_tensor(
+                out=y[:, on_vector],
+                in0=y[:, on_vector],
+                scalar=rstd[i][:],
+                in1=shift_ps[:, on_vector],
+                op0=ALU.mult,
+                op1=ALU.add,
+            )
+            nc.sync.dma_start(out=out_rows[:, half(0)], in_=y[:, half(0)])
+            if is_shared(i):
+                nc.gpsimd.tensor_tensor(out=y[:, half(1)], in0=scaled[i][:], in1=shift_bc[:], op=ALU.add)
+            nc.sync.dma_start(out=out_rows[:, half(1)], in_=y[:, half(1)])
 
         def is_tile(i):
             return 0 <= i < N_TILES
@@ -295,22 +289,22 @@ def tile_swintransformerblock_pa_t_kernel(tc, x, o, out_w, out_b, ln1_g, ln1_b, 
                 mean_tile(s)
             if is_tile(s - 1):
                 gain_tile(s - 1)
-                if is_shared(s - 1):
-                    scale_half(s - 1)
+            if is_tile(s - 2) and is_shared(s - 2):
+                scale_half(s - 2)
             for i in to_turn:
                 regroup_tile(i, turned_tiles[i])
             if is_tile(s):
                 variance_tile(s)
-            if is_tile(s - 1):
-                shift_tile(s - 1)
+            if is_tile(s - 2):
+                shift_tile(s - 2)
             if s >= 0 and is_tile(s + LOAD_LEAD):
                 load_tile(s + LOAD_LEAD)
 
         for s in range(-max(FIRST_TRANSPOSE_LEAD, BIAS_LEAD), 0):
             step(s)
         for h in range(HALVES):
-            nc.tensor.matmul(out=gain_ps[h][:], lhsT=ones[:], rhs=rows[:, GAIN, half(h)], start=True, stop=True)
-            nc.tensor.matmul(out=shift_ps[h][:], lhsT=ones[:], rhs=rows[:, SHIFT, half(h)], start=True, stop=True)
-        nc.scalar.copy(out=shift_bc[:], in_=shift_ps[1][:])
-        for s in range(0, N_TILES + 1):
+            nc.tensor.matmul(out=gain_ps[:, half(h)], lhsT=ones[:], rhs=rows[:, GAIN, half(h)], start=True, stop=True)
+            nc.tensor.matmul(out=shift_ps[:, half(h)], lhsT=ones[:], rhs=rows[:, SHIFT, half(h)], start=True, stop=True)
+        nc.scalar.copy(out=shift_bc[:], in_=shift_ps[:, half(1)])
+        for s in range(0, N_TILES + 2):
             step(s)

@@ -31,7 +31,7 @@ SHIFT = 2
 
 FIRST_TRANSPOSE_LEAD = 3
 TRANSPOSE_LEAD = 5
-QUANTISE_LEAD = 2
+QUANTISE_LEAD = 1
 BAND_QUANTISE_LEAD = 1
 BIAS_LEAD = 2
 SHARED_TILE = 1
@@ -62,34 +62,43 @@ def tile_swintransformerblock_pa_t_kernel(tc, x, o, out_w, out_b, ln1_g, ln1_b, 
         work = ctx.enter_context(tc.tile_pool(name="work", bufs=4))
         small = ctx.enter_context(tc.tile_pool(name="small", bufs=4))
         const_ps = ctx.enter_context(tc.psum_pool(name="const_ps", bufs=1))
-        acc_ps = ctx.enter_context(tc.psum_pool(name="acc_ps", bufs=2))
+        acc_ps = ctx.enter_context(tc.psum_pool(name="acc_ps", bufs=1))
         turn_ps = ctx.enter_context(tc.psum_pool(name="turn_ps", bufs=2))
         ctx.enter_context(tc.manual_schedule())
 
         o_tiles = {}
         x_tiles = {}
 
-        def load_tile(i):
-            j = i % BAND_TILES
+        def load_o(i):
             o_tile = inputs.tile([P, E], BF16, tag="o_tile")
             nc.sync.dma_start(
-                out=o_tile[:], in_=o_tok[band_rows(i), :].rearrange("(p j) e -> p j e", j=BAND_TILES)[:, j, :]
+                out=o_tile[:],
+                in_=o_tok[band_rows(i), :].rearrange("(p j) e -> p j e", j=BAND_TILES)[:, i % BAND_TILES, :],
             )
+            o_tiles[i] = o_tile
+
+        def load_x(i):
             x_tile = inputs.tile([P, E], BF16, tag="x_tile")
             x_runs = x_tok[band_rows(i), :].rearrange("(r w h j) e -> h j w r e", r=8, w=8, h=2, j=BAND_TILES)
             for h in range(2):
-                nc.sync.dma_start(out=x_tile[h:P:2, :], in_=x_runs[h, j])
-            o_tiles[i] = o_tile
+                nc.sync.dma_start(out=x_tile[h:P:2, :], in_=x_runs[h, i % BAND_TILES])
             x_tiles[i] = x_tile
+
+        def load_tile(i):
+            load_o(i)
+            load_x(i)
 
         vectors = consts.tile([1, 3, E], BF16)
         for v, vec in enumerate((out_b, ln1_g, ln1_b)):
             nc.sync.dma_start(out=vectors[0:1, v, :], in_=vec.rearrange("(a e) -> a e", a=1))
+        load_o(0)
         w_raw = weights.tile([P, C_TILES, E], BF16)
         w_view = out_w.rearrange("(c p) k -> p c k", p=P)
         for c in range(C_TILES):
+            if c == C_TILES // 2:
+                load_x(0)
             nc.sync.dma_start(out=w_raw[:, c, :], in_=w_view[:, c, :])
-        for i in range(LOAD_LEAD):
+        for i in range(1, LOAD_LEAD):
             load_tile(i)
 
         ident = consts.tile([P, P], F32)
@@ -117,7 +126,7 @@ def tile_swintransformerblock_pa_t_kernel(tc, x, o, out_w, out_b, ln1_g, ln1_b, 
                 turned = turn_ps.tile([P, WORD_BLOCKS, P], F32, tag="turned")
                 for b in range(WORD_BLOCKS):
                     nc.tensor.transpose(turned[:, b, :], w_words[:, c, b * P : (b + 1) * P], ident[:])
-                copy = nc.scalar.copy if c % 2 == 0 else nc.vector.tensor_copy
+                copy = nc.vector.tensor_copy if c == C_TILES - 1 else nc.scalar.copy
                 copy(
                     out=w_grouped_words[:, :, c * P : (c + 1) * P, :],
                     in_=turned[:].rearrange("p (g u) c -> p g c u", u=2),
@@ -130,14 +139,14 @@ def tile_swintransformerblock_pa_t_kernel(tc, x, o, out_w, out_b, ln1_g, ln1_b, 
                     in_=w_grouped[:, g, channels, :].rearrange("p c f -> p (c f)"),
                 )
 
-        prepare_weights(0)
+        bias_ps = const_ps.tile([P, E], BF16, name="bias_ps")
         bias_bc = consts.tile([P, E], BF16)
-        for h in range(HALVES):
-            bias_ps = acc_ps.tile([P, BANK], F32, tag="acc%d" % h)
-            nc.tensor.matmul(out=bias_ps[:], lhsT=ones[:], rhs=rows[:, BIAS, half(h)], start=True, stop=True)
-            nc.scalar.copy(out=bias_bc[:, half(h)], in_=bias_ps[:])
-        for first in range(W_GROUP, C_TILES, W_GROUP):
-            prepare_weights(first)
+
+        def spread_bias():
+            for h in range(HALVES):
+                nc.tensor.matmul(
+                    out=bias_ps[:, half(h)], lhsT=ones[:], rhs=rows[:, BIAS, half(h)], start=True, stop=True
+                )
 
         gain_ps = const_ps.tile([P, E], BF16, name="gain_ps")
         shift_ps = const_ps.tile([P, E], BF16, name="shift_ps")
@@ -183,34 +192,34 @@ def tile_swintransformerblock_pa_t_kernel(tc, x, o, out_w, out_b, ln1_g, ln1_b, 
             )
 
         def add_bias(i):
-            engine = nc.vector if i < BIAS_LEAD else nc.gpsimd
             xb = work.tile([P, E], F32, tag="x_bias", bufs=BIAS_LEAD)
-            engine.tensor_tensor(out=xb[:], in0=x_tiles[i][:], in1=bias_bc[:], op=ALU.add)
+            if i < BIAS_LEAD:
+                nc.vector.tensor_tensor(out=xb[:], in0=x_tiles[i][:], in1=bias_ps[:], op=ALU.add)
+            else:
+                nc.gpsimd.tensor_tensor(out=xb[:], in0=x_tiles[i][:], in1=bias_bc[:], op=ALU.add)
             x_bias[i] = xb
 
-        def matmul_tile(i):
-            acc[i] = []
-            for h in range(HALVES):
-                bank = acc_ps.tile([P, BANK], F32, tag="acc%d" % h)
-                for g in range(PASSES):
-                    block = (i % BAND_TILES) * PASSES + g
-                    cols = slice(block * P, (block + 1) * P)
-                    nc.tensor.matmul_mx(
-                        out=bank[:],
-                        lhsT=o_codes[i // BAND_TILES][:, cols].bitcast(FP8X4),
-                        lhsT_scale=o_scales[i // BAND_TILES][:, cols],
-                        rhs=w_codes[:, g, half(h)].bitcast(FP8X4),
-                        rhs_scale=w_scales[:, g, half(h)],
-                        start=(g == 0),
-                        stop=(g == PASSES - 1),
-                    )
-                acc[i].append(bank)
+        def matmul_half(i, h):
+            bank = acc_ps.tile([P, BANK], F32, tag="acc%d" % h)
+            for g in range(PASSES):
+                block = (i % BAND_TILES) * PASSES + g
+                cols = slice(block * P, (block + 1) * P)
+                nc.tensor.matmul_mx(
+                    out=bank[:],
+                    lhsT=o_codes[i // BAND_TILES][:, cols].bitcast(FP8X4),
+                    lhsT_scale=o_scales[i // BAND_TILES][:, cols],
+                    rhs=w_codes[:, g, half(h)].bitcast(FP8X4),
+                    rhs_scale=w_scales[:, g, half(h)],
+                    start=(g == 0),
+                    stop=(g == PASSES - 1),
+                )
+            acc[i, h] = bank
 
         def residual_half(i, h):
             if h == 0:
                 resid[i] = work.tile([P, E], F32, tag="resid", name="resid")
             nc.vector.tensor_tensor(
-                out=resid[i][:, half(h)], in0=acc[i][h][:], in1=x_bias[i][:, half(h)], op=ALU.add
+                out=resid[i][:, half(h)], in0=acc[i, h][:], in1=x_bias[i][:, half(h)], op=ALU.add
             )
 
         def mean_tile(i):
@@ -271,9 +280,11 @@ def tile_swintransformerblock_pa_t_kernel(tc, x, o, out_w, out_b, ln1_g, ln1_b, 
 
         def step(s):
             to_turn = [i for i in range(first_to_turn(s), first_to_turn(s + 1)) if is_tile(i)]
-            for i in to_turn:
-                turned_tiles[i] = transpose_tile(i)
-            if is_tile(s):
+            lead_grows = s < TRANSPOSE_LEAD - FIRST_TRANSPOSE_LEAD
+            if not lead_grows:
+                for i in to_turn:
+                    turned_tiles[i] = transpose_tile(i)
+            if is_tile(s) and s > 0:
                 residual_half(s, 0)
             if 0 <= s + QUANTISE_LEAD < BAND_TILES:
                 quantise_tiles(s + QUANTISE_LEAD, 1)
@@ -281,10 +292,16 @@ def tile_swintransformerblock_pa_t_kernel(tc, x, o, out_w, out_b, ln1_g, ln1_b, 
                 quantise_tiles(s + BAND_QUANTISE_LEAD, BAND_TILES)
             if is_tile(s):
                 residual_half(s, 1)
+            if s == 0:
+                add_bias(1)
             if is_tile(s + BIAS_LEAD):
                 add_bias(s + BIAS_LEAD)
             if is_tile(s + 1):
-                matmul_tile(s + 1)
+                for h in range(HALVES):
+                    matmul_half(s + 1, h)
+            if lead_grows:
+                for i in to_turn:
+                    turned_tiles[i] = transpose_tile(i)
             if is_tile(s):
                 mean_tile(s)
             if is_tile(s - 1):
@@ -300,11 +317,27 @@ def tile_swintransformerblock_pa_t_kernel(tc, x, o, out_w, out_b, ln1_g, ln1_b, 
             if s >= 0 and is_tile(s + LOAD_LEAD):
                 load_tile(s + LOAD_LEAD)
 
-        for s in range(-max(FIRST_TRANSPOSE_LEAD, BIAS_LEAD), 0):
-            step(s)
+        def turn_and_regroup(i):
+            regroup_tile(i, transpose_tile(i))
+
+        turn_and_regroup(0)
+        quantise_tiles(0, 1)
+        spread_bias()
+        prepare_weights(0)
+        prepare_weights(2)
+        add_bias(0)
+        prepare_weights(4)
+        matmul_half(0, 0)
+        residual_half(0, 0)
+        prepare_weights(6)
+        turn_and_regroup(1)
+        turn_and_regroup(2)
+        matmul_half(0, 1)
+        nc.scalar.copy(out=bias_bc[:], in_=bias_ps[:])
+        step(0)
         for h in range(HALVES):
             nc.tensor.matmul(out=gain_ps[:, half(h)], lhsT=ones[:], rhs=rows[:, GAIN, half(h)], start=True, stop=True)
             nc.tensor.matmul(out=shift_ps[:, half(h)], lhsT=ones[:], rhs=rows[:, SHIFT, half(h)], start=True, stop=True)
         nc.scalar.copy(out=shift_bc[:], in_=shift_ps[:, half(1)])
-        for s in range(0, N_TILES + 2):
+        for s in range(1, N_TILES + 2):
             step(s)

@@ -265,10 +265,12 @@ def tile_swintransformerblock_pa_t_kernel(tc, x, o, out_w, out_b, ln1_g, ln1_b, 
                 op0=ALU.mult,
                 op1=ALU.add,
             )
-            nc.sync.dma_start(out=out_rows[:, half(0)], in_=y[:, half(0)])
             if is_shared(i):
+                nc.sync.dma_start(out=out_rows[:, half(0)], in_=y[:, half(0)])
                 nc.gpsimd.tensor_tensor(out=y[:, half(1)], in0=scaled[i][:], in1=shift_bc[:], op=ALU.add)
-            nc.sync.dma_start(out=out_rows[:, half(1)], in_=y[:, half(1)])
+                nc.sync.dma_start(out=out_rows[:, half(1)], in_=y[:, half(1)])
+            else:
+                nc.sync.dma_start(out=out_rows, in_=y[:])
 
         def is_tile(i):
             return 0 <= i < N_TILES

from contextlib import ExitStack

import concourse.mybir as mybir
from concourse.masks import make_identity

F32 = mybir.dt.float32
BF16 = mybir.dt.bfloat16
U32 = mybir.dt.uint32
U8 = mybir.dt.uint8
FP8X4 = mybir.dt.float8_e4m3fn_x4
ALU = mybir.AluOpType
ACT = mybir.ActivationFunctionType

P = 128
E = 1024
N_TOKENS = 4096
BAND_TOKENS = 512
BAND_TILES = BAND_TOKENS // P
N_TILES = N_TOKENS // P
PACK = 4
PASSES = E // (P * PACK)
WORD_BLOCKS = E // 2 // P
BANK = 512
HALVES = E // BANK
C_TILES = E // P
W_GROUP = 2
LN_EPS = 1e-5
BIAS = 0
GAIN = 1
SHIFT = 2

FIRST_TRANSPOSE_LEAD = 3
TRANSPOSE_LEAD = 5
QUANTISE_LEAD = 1
BAND_QUANTISE_LEAD = 1
BIAS_LEAD = 2
SHARED_TILE = 1
LOAD_LEAD = 8

FLOPS = 2 * N_TOKENS * E * E


def half(h):
    return slice(h * BANK, (h + 1) * BANK)


def tile_swintransformerblock_pa_t_kernel(tc, x, o, out_w, out_b, ln1_g, ln1_b, out):
    nc = tc.nc
    x_tok = x.rearrange("b t e -> (b t) e")
    o_tok = o.rearrange("l n e -> (l n) e")
    out_tok = out.rearrange("l n e -> (l n) e")

    def band_rows(i):
        band = i // BAND_TILES
        return slice(band * BAND_TOKENS, (band + 1) * BAND_TOKENS)

    with ExitStack() as ctx:
        consts = ctx.enter_context(tc.tile_pool(name="consts", bufs=1))
        weights = ctx.enter_context(tc.tile_pool(name="weights", bufs=1))
        inputs = ctx.enter_context(tc.tile_pool(name="inputs", bufs=LOAD_LEAD))
        operands = ctx.enter_context(tc.tile_pool(name="operands", bufs=2))
        work = ctx.enter_context(tc.tile_pool(name="work", bufs=4))
        small = ctx.enter_context(tc.tile_pool(name="small", bufs=4))
        const_ps = ctx.enter_context(tc.psum_pool(name="const_ps", bufs=1))
        acc_ps = ctx.enter_context(tc.psum_pool(name="acc_ps", bufs=1))
        turn_ps = ctx.enter_context(tc.psum_pool(name="turn_ps", bufs=2))
        ctx.enter_context(tc.manual_schedule())

        o_tiles = {}
        x_tiles = {}

        def load_o(i):
            o_tile = inputs.tile([P, E], BF16, tag="o_tile")
            nc.sync.dma_start(
                out=o_tile[:],
                in_=o_tok[band_rows(i), :].rearrange("(p j) e -> p j e", j=BAND_TILES)[:, i % BAND_TILES, :],
            )
            o_tiles[i] = o_tile

        def load_x(i):
            x_tile = inputs.tile([P, E], BF16, tag="x_tile")
            x_runs = x_tok[band_rows(i), :].rearrange("(r w h j) e -> h j w r e", r=8, w=8, h=2, j=BAND_TILES)
            for h in range(2):
                nc.sync.dma_start(out=x_tile[h:P:2, :], in_=x_runs[h, i % BAND_TILES])
            x_tiles[i] = x_tile

        def load_tile(i):
            load_o(i)
            load_x(i)

        vectors = consts.tile([1, 3, E], BF16)
        for v, vec in enumerate((out_b, ln1_g, ln1_b)):
            nc.sync.dma_start(out=vectors[0:1, v, :], in_=vec.rearrange("(a e) -> a e", a=1))
        load_o(0)
        w_raw = weights.tile([P, C_TILES, E], BF16)
        w_view = out_w.rearrange("(c p) k -> p c k", p=P)
        for c in range(C_TILES):
            if c == C_TILES // 2:
                load_x(0)
            nc.sync.dma_start(out=w_raw[:, c, :], in_=w_view[:, c, :])
        for i in range(1, LOAD_LEAD):
            load_tile(i)

        ident = consts.tile([P, P], F32)
        make_identity(nc, ident[:])
        ones = consts.tile([P, P], BF16)
        nc.vector.memset(ones[:], 1.0)
        eps = consts.tile([P, 1], F32)
        nc.vector.memset(eps[:], LN_EPS)
        warm = consts.tile([P, 1], F32)
        nc.scalar.activation(out=warm[:], in_=eps[:], func=ACT.Abs_reciprocal_sqrt)

        rows = consts.tile([P, 3, E], BF16)
        for v in (BIAS, GAIN, SHIFT):
            nc.vector.memset(rows[:, v, :], 0.0)
            nc.vector.tensor_copy(out=rows[0:1, v, :], in_=vectors[0:1, v, :])

        w_words = w_raw[:].bitcast(F32)
        w_grouped = weights.tile([P, PASSES, E, PACK], BF16, align_bytes=64)
        w_grouped_words = w_grouped[:].bitcast(F32)
        w_codes = weights.tile([P, PASSES, E], U32, align_bytes=64)
        w_scales = weights.tile([P, PASSES, E], U8, align_bytes=64)

        def prepare_weights(first):
            for c in range(first, first + W_GROUP):
                turned = turn_ps.tile([P, WORD_BLOCKS, P], F32, tag="turned")
                for b in range(WORD_BLOCKS):
                    nc.tensor.transpose(turned[:, b, :], w_words[:, c, b * P : (b + 1) * P], ident[:])
                copy = nc.vector.tensor_copy if c == C_TILES - 1 else nc.scalar.copy
                copy(
                    out=w_grouped_words[:, :, c * P : (c + 1) * P, :],
                    in_=turned[:].rearrange("p (g u) c -> p g c u", u=2),
                )
            channels = slice(first * P, (first + W_GROUP) * P)
            for g in range(PASSES):
                nc.vector.quantize_mx(
                    out=w_codes[:, g, channels].bitcast(FP8X4),
                    scales=w_scales[:, g, channels],
                    in_=w_grouped[:, g, channels, :].rearrange("p c f -> p (c f)"),
                )

        bias_ps = const_ps.tile([P, E], BF16, name="bias_ps")
        bias_bc = consts.tile([P, E], BF16)

        def spread_bias():
            for h in range(HALVES):
                nc.tensor.matmul(
                    out=bias_ps[:, half(h)], lhsT=ones[:], rhs=rows[:, BIAS, half(h)], start=True, stop=True
                )

        gain_ps = const_ps.tile([P, E], BF16, name="gain_ps")
        shift_ps = const_ps.tile([P, E], BF16, name="shift_ps")
        shift_bc = consts.tile([P, BANK], BF16)
        gained = {}
        scaled = {}
        grouped_bands = {}
        o_codes = {}
        o_scales = {}
        x_bias = {}
        acc = {}
        resid = {}
        neg_mean = {}
        rstd = {}

        def transpose_tile(i):
            turned = turn_ps.tile([P, WORD_BLOCKS, P], F32, tag="turned")
            o_words = o_tiles[i][:].bitcast(F32)
            for b in range(WORD_BLOCKS):
                nc.tensor.transpose(turned[:, b, :], o_words[:, b * P : (b + 1) * P], ident[:])
            return turned

        def regroup_tile(i, turned):
            band, j = divmod(i, BAND_TILES)
            if j == 0:
                grouped_bands[band] = operands.tile(
                    [P, BAND_TILES, PASSES, P, PACK], BF16, tag="grouped", name="grouped", align_bytes=64
                )
            nc.scalar.copy(
                out=grouped_bands[band][:, j, :, :, :].bitcast(F32), in_=turned[:].rearrange("p (g u) t -> p g t u", u=2)
            )

        def quantise_tiles(first, count):
            band, j = divmod(first, BAND_TILES)
            if j == 0:
                o_codes[band] = operands.tile([P, BAND_TILES * PASSES * P], U32, tag="codes", name="codes", align_bytes=64)
                o_scales[band] = operands.tile([P, BAND_TILES * PASSES * P], U8, tag="scales", name="scales", align_bytes=64)
            cols = slice(j * PASSES * P, (j + count) * PASSES * P)
            nc.vector.quantize_mx(
                out=o_codes[band][:, cols].bitcast(FP8X4),
                scales=o_scales[band][:, cols],
                in_=grouped_bands[band][:, j : j + count, :, :, :].rearrange("p j g t f -> p (j g t f)"),
            )

        def add_bias(i):
            xb = work.tile([P, E], F32, tag="x_bias", bufs=BIAS_LEAD)
            if i < BIAS_LEAD:
                nc.vector.tensor_tensor(out=xb[:], in0=x_tiles[i][:], in1=bias_ps[:], op=ALU.add)
            else:
                nc.gpsimd.tensor_tensor(out=xb[:], in0=x_tiles[i][:], in1=bias_bc[:], op=ALU.add)
            x_bias[i] = xb

        def matmul_half(i, h):
            bank = acc_ps.tile([P, BANK], F32, tag="acc%d" % h)
            for g in range(PASSES):
                block = (i % BAND_TILES) * PASSES + g
                cols = slice(block * P, (block + 1) * P)
                nc.tensor.matmul_mx(
                    out=bank[:],
                    lhsT=o_codes[i // BAND_TILES][:, cols].bitcast(FP8X4),
                    lhsT_scale=o_scales[i // BAND_TILES][:, cols],
                    rhs=w_codes[:, g, half(h)].bitcast(FP8X4),
                    rhs_scale=w_scales[:, g, half(h)],
                    start=(g == 0),
                    stop=(g == PASSES - 1),
                )
            acc[i, h] = bank

        def residual_half(i, h):
            if h == 0:
                resid[i] = work.tile([P, E], F32, tag="resid", name="resid")
            nc.vector.tensor_tensor(
                out=resid[i][:, half(h)], in0=acc[i, h][:], in1=x_bias[i][:, half(h)], op=ALU.add
            )

        def mean_tile(i):
            unread = work.tile([P, E], BF16, tag="unread_scaled")
            nm = small.tile([P, 1], F32, tag="neg_mean")
            nc.scalar.activation(out=unread[:], in_=resid[i][:], func=ACT.Identity, scale=-1.0 / E, accum_out=nm[:])
            neg_mean[i] = nm

        def variance_tile(i):
            unread = work.tile([P, E], BF16, tag="unread_squares")
            ssq = small.tile([P, 1], F32, tag="ssq")
            nc.scalar.activation(
                out=unread[:], in_=resid[i][:], func=ACT.Square, bias=neg_mean[i][:], accum_out=ssq[:]
            )
            rs = small.tile([P, 1], F32, tag="rstd")
            nc.scalar.activation(out=rs[:], in_=ssq[:], func=ACT.Abs_reciprocal_sqrt, bias=eps[:], scale=1.0 / E)
            rstd[i] = rs

        def is_shared(i):
            return i % BAND_TILES == SHARED_TILE

        def gain_tile(i):
            y = work.tile([P, E], F32, tag="y")
            gained[i] = y
            nc.vector.scalar_tensor_tensor(
                out=y[:], in0=resid[i][:], scalar=neg_mean[i][:], in1=gain_ps[:], op0=ALU.add, op1=ALU.mult
            )

        def scale_half(i):
            sc = work.tile([P, BANK], F32, tag="scaled", bufs=2)
            nc.scalar.activation(out=sc[:], in_=gained[i][:, half(1)], func=ACT.Identity, scale=rstd[i][:])
            scaled[i] = sc

        def shift_tile(i):
            y = gained[i]
            out_rows = out_tok[band_rows(i), :].rearrange("(p j) e -> p j e", j=BAND_TILES)[:, i % BAND_TILES, :]
            on_vector = half(0) if is_shared(i) else slice(0, E)
            nc.vector.scalar_tensor_tensor(
                out=y[:, on_vector],
                in0=y[:, on_vector],
                scalar=rstd[i][:],
                in1=shift_ps[:, on_vector],
                op0=ALU.mult,
                op1=ALU.add,
            )
            if is_shared(i):
                nc.sync.dma_start(out=out_rows[:, half(0)], in_=y[:, half(0)])
                nc.gpsimd.tensor_tensor(out=y[:, half(1)], in0=scaled[i][:], in1=shift_bc[:], op=ALU.add)
                nc.sync.dma_start(out=out_rows[:, half(1)], in_=y[:, half(1)])
            else:
                nc.sync.dma_start(out=out_rows, in_=y[:])

        def is_tile(i):
            return 0 <= i < N_TILES

        turned_tiles = {}

        def first_to_turn(s):
            return s + FIRST_TRANSPOSE_LEAD + min(max(s, 0), TRANSPOSE_LEAD - FIRST_TRANSPOSE_LEAD)

        def step(s):
            to_turn = [i for i in range(first_to_turn(s), first_to_turn(s + 1)) if is_tile(i)]
            lead_grows = s < TRANSPOSE_LEAD - FIRST_TRANSPOSE_LEAD
            if not lead_grows:
                for i in to_turn:
                    turned_tiles[i] = transpose_tile(i)
            if is_tile(s) and s > 0:
                residual_half(s, 0)
            if 0 <= s + QUANTISE_LEAD < BAND_TILES:
                quantise_tiles(s + QUANTISE_LEAD, 1)
            elif is_tile(s + BAND_QUANTISE_LEAD) and (s + BAND_QUANTISE_LEAD) % BAND_TILES == 0:
                quantise_tiles(s + BAND_QUANTISE_LEAD, BAND_TILES)
            if is_tile(s):
                residual_half(s, 1)
            if s == 0:
                add_bias(1)
            if is_tile(s + BIAS_LEAD):
                add_bias(s + BIAS_LEAD)
            if is_tile(s + 1):
                for h in range(HALVES):
                    matmul_half(s + 1, h)
            if lead_grows:
                for i in to_turn:
                    turned_tiles[i] = transpose_tile(i)
            if is_tile(s):
                mean_tile(s)
            if is_tile(s - 1):
                gain_tile(s - 1)
            if is_tile(s - 2) and is_shared(s - 2):
                scale_half(s - 2)
            for i in to_turn:
                regroup_tile(i, turned_tiles[i])
            if is_tile(s):
                variance_tile(s)
            if is_tile(s - 2):
                shift_tile(s - 2)
            if s >= 0 and is_tile(s + LOAD_LEAD):
                load_tile(s + LOAD_LEAD)

        def turn_and_regroup(i):
            regroup_tile(i, transpose_tile(i))

        turn_and_regroup(0)
        quantise_tiles(0, 1)
        spread_bias()
        prepare_weights(0)
        prepare_weights(2)
        add_bias(0)
        prepare_weights(4)
        matmul_half(0, 0)
        residual_half(0, 0)
        prepare_weights(6)
        turn_and_regroup(1)
        turn_and_regroup(2)
        matmul_half(0, 1)
        nc.scalar.copy(out=bias_bc[:], in_=bias_ps[:])
        step(0)
        for h in range(HALVES):
            nc.tensor.matmul(out=gain_ps[:, half(h)], lhsT=ones[:], rhs=rows[:, GAIN, half(h)], start=True, stop=True)
            nc.tensor.matmul(out=shift_ps[:, half(h)], lhsT=ones[:], rhs=rows[:, SHIFT, half(h)], start=True, stop=True)
        nc.scalar.copy(out=shift_bc[:], in_=shift_ps[:, half(1)])
        for s in range(1, N_TILES + 2):
            step(s)
